import numpy as np
import ml_dtypes


def mxq(x, axis, fmt="e4m3"):
    dtype, down = {"e4m3": (ml_dtypes.float8_e4m3fn, 7), "e5m2": (ml_dtypes.float8_e5m2, 14)}[fmt]
    v = np.moveaxis(np.asarray(x, np.float32).astype(ml_dtypes.bfloat16).astype(np.float64), axis, -1)
    blocks = v.reshape(v.shape[:-1] + (-1, 32))
    amax = np.abs(blocks).max(-1, keepdims=True)
    byte = np.maximum(np.where(amax > 0, np.frexp(amax)[1] - 1 + 127, 0) - down, 1)
    scale = np.exp2(byte - 127.0)
    codes = (blocks / scale).astype(np.float32).astype(dtype).astype(np.float64)
    return np.moveaxis((codes * scale).reshape(v.shape), -1, axis)


WIDE = False


def mx_kscale(k):
    if not WIDE:
        return np.ones(k)
    levels = np.array([10, -10, 5, -5, 0])
    a = np.random.permutation(np.resize(levels, k // 512 * 4)).reshape(k // 512, 4)
    idx = np.arange(k)
    return np.exp2(a[idx // 512, idx % 128 // 32])


BF16 = ml_dtypes.bfloat16


def bf(x):
    return np.asarray(x, np.float32).astype(BF16)


def f64(x):
    return np.asarray(x).astype(np.float64)


E2M1 = np.array([0.0, 0.5, 1.0, 1.5, 2.0, 3.0, 4.0, 6.0, -0.0, -0.5, -1.0, -1.5, -2.0, -3.0, -4.0, -6.0])


def pack_weight(w, fmt):
    k, n = w.shape
    w = f64(bf(w)).reshape(k // 32, 32, n)
    amax = np.abs(w).max(1)
    if fmt == "e4m3":
        byte = np.frexp(amax)[1] - 1 + 127 - 7
    else:
        mant, ex = np.frexp(amax / 6.0)
        byte = np.where(mant > 0.5, ex, ex - 1) + 127
    byte = np.clip(np.where(amax > 0, byte, 1), 1, 254)
    scaled = (w * np.exp2(127.0 - byte)[:, None, :]).reshape(k, n).astype(np.float32)
    by_word = np.ascontiguousarray(scaled.reshape(k // 512, 128, 4, n).transpose(0, 1, 3, 2))
    if fmt == "e4m3":
        words = by_word.astype(ml_dtypes.float8_e4m3fn).view(np.uint8)
    else:
        c = by_word.astype(ml_dtypes.float4_e2m1fn).view(np.uint8) & 0xF
        words = c[..., 0::2] | (c[..., 1::2] << 4)
    return np.ascontiguousarray(words), np.ascontiguousarray(byte.astype(np.uint8).reshape(k // 512, 16, n))


def unpack_weight(words, scales, fmt):
    g, p, n, _ = words.shape
    if fmt == "e4m3":
        vals = np.ascontiguousarray(words).view(ml_dtypes.float8_e4m3fn).astype(np.float64)
    else:
        nib = np.empty((g, p, n, 4), np.uint8)
        nib[..., 0::2] = words & 0xF
        nib[..., 1::2] = words >> 4
        vals = E2M1[nib]
    vals = vals * np.repeat(np.exp2(scales.astype(np.float64) - 127.0), 8, axis=1)[..., None]
    return vals.transpose(0, 1, 3, 2).reshape(g * 512, n)

def pack4(w):
    words, scales = pack_weight(w, "e2m1")
    return words.reshape(words.shape[0], 128, -1), scales


def unpack4(words, scales):
    return unpack_weight(words.reshape(words.shape[0], 128, -1, 2), scales, "e2m1")


B, L, C, H, BLK = 2, 512, 1024, 16, 128
D = C // H
MAX_SCALE_MUL = np.log(100.0)
EPS = 1e-12


def l2norm(t):
    n = np.sqrt(np.sum(t * t, axis=-1, keepdims=True))
    return t / np.maximum(n, EPS)


def setup_inputs():
    s = mx_kscale(C)
    lsm = np.linspace(np.log(4.0), MAX_SCALE_MUL + 1.0, H) + 0.05 * np.random.standard_normal(H)
    x = bf(np.random.standard_normal((B, L, C)) * s)
    w = np.random.standard_normal((3 * C, C)) / np.sqrt(C) / s[None, :]
    words, scales = pack4(np.ascontiguousarray(w.T))
    q_bias = bf(np.random.standard_normal(C) * 0.3)
    v_bias = bf(np.random.standard_normal(C) * 0.3)
    return {"x": x,
            "W_qkv_words": words,
            "W_qkv_scales": scales,
            "q_bias": q_bias,
            "v_bias": v_bias,
            "log_scale_mul": bf(lsm.reshape(1, H, 1, 1))}


def reference(x, W_qkv_words, W_qkv_scales, q_bias, v_bias, log_scale_mul):
    qb = f64(q_bias)
    bias = np.concatenate([qb, np.zeros_like(qb), f64(v_bias)])
    qkv = (mxq(f64(x), 2, "e4m3") @ unpack4(W_qkv_words, W_qkv_scales)) + bias
    qkv = qkv.reshape(B, L, 3, H, D)
    q, k, v = np.moveaxis(qkv, 2, 0)
    q = np.swapaxes(q, 1, 2)
    k = np.swapaxes(k, 1, 2)
    v = np.swapaxes(v, 1, 2)
    scale_mul = np.exp(np.minimum(f64(log_scale_mul), MAX_SCALE_MUL))
    q = l2norm(q) * scale_mul
    k = l2norm(k)
    return q, k, v

@@ -1,0 +1,230 @@
+import concourse.mybir as mybir
+from concourse.masks import make_identity
+
+F32 = mybir.dt.float32
+BF16 = mybir.dt.bfloat16
+I32 = mybir.dt.int32
+U32 = mybir.dt.uint32
+U8 = mybir.dt.uint8
+FP8X4 = mybir.dt.float8_e4m3fn_x4
+FP4X4 = mybir.dt.float4_e2m1fn_x4
+ALU = mybir.AluOpType
+ACT = mybir.ActivationFunctionType
+
+P = 128
+B, L, C, H, D = 2, 512, 1024, 16, 64
+K_PASS = 512
+PASSES = C // K_PASS
+TOKENS_PER_PARTITION = B * L // P
+PAIR = 2 * D
+HEAD_PAIRS = H // 2
+BANK_TILES = 4
+HALVES = TOKENS_PER_PARTITION // BANK_TILES
+MAX_SCALE = 100.0
+EPS_SQUARED = 1.0e-24
+
+FLOPS = 2 * B * L * C * 3 * C
+
+
+def tile_selfattention_pa_kernel(
+    tc, x, W_qkv_words, W_qkv_scales, q_bias, v_bias, log_scale_mul, out_0, out_1, out_2
+):
+    nc = tc.nc
+    with tc.tile_pool(name="keep", bufs=1) as keep, tc.tile_pool(
+        name="regroup", bufs=2
+    ) as regroup, tc.tile_pool(name="stage", bufs=12) as stage, tc.tile_pool(
+        name="small", bufs=4
+    ) as small, tc.psum_pool(name="psum", bufs=4) as psum:
+        rows = keep.tile([P, 2 * C + D], BF16)
+        nc.vector.memset(rows[:].bitcast(I32), 0)
+        w_planes = keep.tile([P, PASSES, 3 * C], U8, align_bytes=64)
+        nc.vector.memset(w_planes[:].rearrange("p g n -> p (g n)").bitcast(I32), 0)
+        ones = keep.tile([P, P], BF16)
+        nc.vector.memset(ones[:], 1.0)
+        ident = keep.tile([P, P], F32)
+        make_identity(nc, ident[:])
+
+        x_sb = keep.tile([P, TOKENS_PER_PARTITION, C], BF16)
+        x_view = x.rearrange("b (p j) c -> p b (j c)", j=TOKENS_PER_PARTITION)
+        for chunk in range(4):
+            nc.sync.dma_start(
+                out=x_sb[:, 2 * chunk : 2 * chunk + 2, :].rearrange("p j c -> p (j c)"),
+                in_=x_view[:, :, 2 * C * chunk : 2 * C * (chunk + 1)],
+            )
+        nc.scalar.dma_start(out=rows[0:1, 0:C], in_=q_bias.rearrange("(o n) -> o n", o=1))
+        nc.scalar.dma_start(out=rows[0:1, C : 2 * C], in_=v_bias.rearrange("(o n) -> o n", o=1))
+        nc.scalar.dma_start(
+            out=rows[0:1, 2 * C : 2 * C + H],
+            in_=log_scale_mul.rearrange("a h b c -> a (h b c)"),
+        )
+        for r in range(4):
+            nc.sync.dma_start(
+                out=w_planes[r:P:32, :, :].bitcast(I32),
+                in_=W_qkv_scales[:, r:16:4, :].rearrange("g q n -> q g n").bitcast(I32),
+            )
+        w_words = keep.tile([P, PASSES, 2 * 3 * C], U8, align_bytes=64)
+        w_view = W_qkv_words.rearrange("g p n -> p g n")
+        for half in range(2):
+            for tensor in range(3):
+                first = 2 * (C * tensor + (C // 2) * half)
+                nc.sync.dma_start(
+                    out=w_words[:, :, first : first + C].bitcast(I32),
+                    in_=w_view[:, :, first : first + C].bitcast(I32),
+                )
+
+        x_words = x_sb[:].bitcast(F32)
+        x_codes = keep.tile([P, TOKENS_PER_PARTITION, PASSES, P], U32, align_bytes=64)
+        x_planes = keep.tile([P, TOKENS_PER_PARTITION, PASSES, P], U8, align_bytes=64)
+        for chunk in range(4):
+            grouped = regroup.tile([P, 2, 2 * K_PASS], BF16, align_bytes=64)
+            for jj in range(2):
+                j = 2 * chunk + jj
+                flipped = psum.tile([P, PASSES, 2, P], F32, tag=("brief" if jj == 0 else "held"))
+                for g in range(PASSES):
+                    for u in range(2):
+                        nc.tensor.transpose(
+                            flipped[:, g, u, :],
+                            x_words[:, j, 256 * g + u : 256 * (g + 1) : 2],
+                            ident[:],
+                        )
+                target = grouped[:, jj, :].bitcast(F32).rearrange(
+                    "p (g m u) -> p g m u", g=PASSES, u=2
+                )
+                source = flipped[:].rearrange("p g u m -> p g m u")
+                if jj == 0:
+                    nc.vector.tensor_copy(out=target, in_=source)
+                else:
+                    nc.scalar.copy(out=target, in_=source)
+            nc.vector.quantize_mx(
+                out=x_codes[:, 2 * chunk : 2 * chunk + 2, :, :]
+                .rearrange("p j g m -> p (j g m)")
+                .bitcast(FP8X4),
+                scales=x_planes[:, 2 * chunk : 2 * chunk + 2, :, :].rearrange("p j g m -> p (j g m)"),
+                in_=grouped[:].rearrange("p j c -> p (j c)"),
+            )
+
+        bias_sb = keep.tile([P, 2 * C], F32)
+        for piece in range(4):
+            spread = psum.tile([P, 512], F32, tag="brief")
+            nc.tensor.matmul(
+                spread[:], lhsT=ones[:], rhs=rows[:, 512 * piece : 512 * (piece + 1)],
+                start=True, stop=True,
+            )
+            nc.scalar.copy(out=bias_sb[:, 512 * piece : 512 * (piece + 1)], in_=spread[:])
+        spread = psum.tile([P, 512], F32, tag="held")
+        nc.tensor.matmul(
+            spread[:, 0:D], lhsT=ones[:], rhs=rows[:, 2 * C : 2 * C + D], start=True, stop=True
+        )
+        scale_raw = keep.tile([P, H], F32)
+        nc.scalar.activation(out=scale_raw[:], in_=spread[:, 0:H], func=ACT.Exp)
+        scale_mul = keep.tile([P, H], F32)
+        nc.vector.tensor_scalar_min(out=scale_mul[:], in0=scale_raw[:], scalar1=MAX_SCALE)
+
+        def project(first_column, tag):
+            banks = []
+            for half in range(HALVES):
+                bank = psum.tile([P, BANK_TILES, PAIR], F32, tag=tag, name="bank")
+                for jj in range(BANK_TILES):
+                    j = BANK_TILES * half + jj
+                    for g in range(PASSES):
+                        nc.tensor.matmul_mx(
+                            out=bank[:, jj, :],
+                            lhsT=x_codes[:, j, g, :].bitcast(FP8X4),
+                            lhsT_scale=x_planes[:, j, g, :],
+                            rhs=w_words[:, g, 2 * first_column : 2 * (first_column + PAIR)].bitcast(FP4X4),
+                            rhs_scale=w_planes[:, g, first_column : first_column + PAIR],
+                            start=(g == 0),
+                            stop=(g == PASSES - 1),
+                        )
+                banks.append(bank)
+            return banks
+
+        def by_token_tile(result, half):
+            return result[:, :, BANK_TILES * half : BANK_TILES * (half + 1), :].rearrange(
+                "p h j d -> p j h d"
+            )
+
+        def add_bias(banks, bias_columns):
+            result = stage.tile([P, 2, TOKENS_PER_PARTITION, D], F32, tag="result", name="result")
+            for half in range(HALVES):
+                nc.vector.tensor_tensor(
+                    out=by_token_tile(result, half),
+                    in0=banks[half][:].rearrange("p j (h d) -> p j h d", h=2),
+                    in1=bias_columns.rearrange("p (h d) -> p h d", h=2)
+                    .unsqueeze(1)
+                    .to_broadcast([P, BANK_TILES, 2, D]),
+                    op=ALU.add,
+                )
+            return result
+
+        def inverse_norms(head_of):
+            squares = small.tile([P, 2, TOKENS_PER_PARTITION], F32, tag="squares", name="squares")
+            for j in range(TOKENS_PER_PARTITION):
+                for h in range(2):
+                    unused = small.tile([P, D], BF16, tag="unused", name="unused")
+                    nc.scalar.activation(
+                        out=unused[:], in_=head_of(h, j), func=ACT.Square,
+                        accum_out=squares[:, h, j : j + 1],
+                    )
+            excess = small.tile([P, 2, TOKENS_PER_PARTITION], F32, tag="excess", name="excess")
+            nc.scalar.activation(out=excess[:], in_=squares[:], func=ACT.Relu, bias=-EPS_SQUARED)
+            inverse = small.tile([P, 2, TOKENS_PER_PARTITION], F32, tag="inverse", name="inverse")
+            nc.scalar.activation(
+                out=inverse[:], in_=excess[:], func=ACT.Abs_reciprocal_sqrt, bias=EPS_SQUARED
+            )
+            return inverse
+
+        def store(out, pair, result):
+            view = out.rearrange("b h (p j) d -> h p b (j d)", j=TOKENS_PER_PARTITION)
+            for h in range(2):
+                nc.sync.dma_start(
+                    out=view[2 * pair + h], in_=result[:, h, :, :].rearrange("p j d -> p (j d)")
+                )
+
+        def front(pair):
+            q_raw = add_bias(project(PAIR * pair, "brief"), bias_sb[:, PAIR * pair : PAIR * (pair + 1)])
+            k_banks = project(C + PAIR * pair, "held")
+            v = add_bias(
+                project(2 * C + PAIR * pair, "brief"), bias_sb[:, C + PAIR * pair : C + PAIR * (pair + 1)]
+            )
+            store(out_2, pair, v)
+            q_inverse = inverse_norms(lambda h, j: q_raw[:, h, j, :])
+            k_inverse = inverse_norms(
+                lambda h, j: k_banks[j // BANK_TILES][:, j % BANK_TILES, D * h : D * (h + 1)]
+            )
+            return q_raw, q_inverse, k_banks, k_inverse
+
+        def back(pair, q_raw, q_inverse, k_banks, k_inverse):
+            q_factor = small.tile([P, 2, TOKENS_PER_PARTITION], F32, tag="q_factor", name="q_factor")
+            nc.gpsimd.tensor_tensor(
+                out=q_factor[:], in0=q_inverse[:],
+                in1=scale_mul[:, 2 * pair : 2 * pair + 2].unsqueeze(2).to_broadcast([P, 2, TOKENS_PER_PARTITION]),
+                op=ALU.mult,
+            )
+            for h in range(2):
+                nc.gpsimd.tensor_tensor(
+                    out=q_raw[:, h, :, :], in0=q_raw[:, h, :, :],
+                    in1=q_factor[:, h, :].unsqueeze(2).to_broadcast([P, TOKENS_PER_PARTITION, D]),
+                    op=ALU.mult,
+                )
+            k = stage.tile([P, 2, TOKENS_PER_PARTITION, D], F32, tag="result", name="k")
+            for half in range(HALVES):
+                nc.vector.tensor_tensor(
+                    out=by_token_tile(k, half),
+                    in0=k_banks[half][:].rearrange("p j (h d) -> p j h d", h=2),
+                    in1=k_inverse[:, :, BANK_TILES * half : BANK_TILES * (half + 1)]
+                    .rearrange("p h j -> p j h")
+                    .unsqueeze(3)
+                    .to_broadcast([P, BANK_TILES, 2, D]),
+                    op=ALU.mult,
+                )
+            store(out_1, pair, k)
+            store(out_0, pair, q_raw)
+
+        waiting = None
+        for pair in range(HEAD_PAIRS):
+            fresh = front(pair)
+            if waiting is not None:
+                back(pair - 1, *waiting)
+            waiting = fresh
+        back(HEAD_PAIRS - 1, *waiting)

@@ -10,18 +10,31 @@ FP8X4 = mybir.dt.float8_e4m3fn_x4
 FP4X4 = mybir.dt.float4_e2m1fn_x4
 ALU = mybir.AluOpType
 ACT = mybir.ActivationFunctionType
+AX = mybir.AxisListType
 
 P = 128
 B, L, C, H, D = 2, 512, 1024, 16, 64
 K_PASS = 512
 PASSES = C // K_PASS
-TOKENS_PER_PARTITION = B * L // P
+TOKENS = L // P
+TILES = B * TOKENS
 PAIR = 2 * D
-HEAD_PAIRS = H // 2
-BANK_TILES = 4
-HALVES = TOKENS_PER_PARTITION // BANK_TILES
+PAIRS = H // 2
+UNITS = B * PAIRS
+BANK = TOKENS * PAIR
+SUMS = 2 * TOKENS
+Q, K, V = 0, 1, 2
 MAX_SCALE = 100.0
-EPS_SQUARED = 1.0e-24
+INV_EPS = 1.0e12
+TINY = 1.0e-30
+
+NARROW_K = ()
+FOLD = True
+LEAD_K, LEAD_Q, LEAD_V = 0, 0, -1
+NO_FOLD_FROM = 15
+LATER_BIAS = {}
+FLIP_AT = {2: 4, 3: 5, 4: 6, 5: 7}
+VEC_COPY = (0, 2)
 
 FLOPS = 2 * B * L * C * 3 * C
 
@@ -30,12 +43,16 @@ def tile_selfattention_pa_kernel(
     tc, x, W_qkv_words, W_qkv_scales, q_bias, v_bias, log_scale_mul, out_0, out_1, out_2
 ):
     nc = tc.nc
-    with tc.tile_pool(name="keep", bufs=1) as keep, tc.tile_pool(
-        name="regroup", bufs=2
-    ) as regroup, tc.tile_pool(name="stage", bufs=12) as stage, tc.tile_pool(
-        name="small", bufs=4
-    ) as small, tc.psum_pool(name="psum", bufs=4) as psum:
-        rows = keep.tile([P, 2 * C + D], BF16)
+    outs = (out_0, out_1, out_2)
+    with tc.tile_pool(name="keep", bufs=1) as keep, tc.tile_pool(name="regroup", bufs=4) as regroup, tc.tile_pool(
+        name="stage", bufs=12
+    ) as stage, tc.tile_pool(name="scratch", bufs=3) as scratch, tc.tile_pool(name="small", bufs=4) as small, tc.psum_pool(
+        name="psum", bufs=5
+    ) as psum, tc.psum_pool(name="psum_k", bufs=3) as psum_k:
+        warm = keep.tile([P, 4], F32)
+        nc.vector.memset(warm[:], 1.0)
+        nc.scalar.activation(out=warm[:, 1:2], in_=warm[:, 0:1], func=ACT.Exp)
+        rows = keep.tile([P, 2 * C], BF16)
         nc.vector.memset(rows[:].bitcast(I32), 0)
         w_planes = keep.tile([P, PASSES, 3 * C], U8, align_bytes=64)
         nc.vector.memset(w_planes[:].rearrange("p g n -> p (g n)").bitcast(I32), 0)
@@ -43,188 +60,267 @@ def tile_selfattention_pa_kernel(
         nc.vector.memset(ones[:], 1.0)
         ident = keep.tile([P, P], F32)
         make_identity(nc, ident[:])
+        multiplier = keep.tile([P, PAIRS, 2 * SUMS], F32)
+        nc.gpsimd.memset(multiplier[:], 1.0)
 
-        x_sb = keep.tile([P, TOKENS_PER_PARTITION, C], BF16)
-        x_view = x.rearrange("b (p j) c -> p b (j c)", j=TOKENS_PER_PARTITION)
-        for chunk in range(4):
+        x_sb = keep.tile([P, TILES, C], BF16)
+        x_view = x.rearrange("b (p j) c -> b p (j c)", j=TOKENS)
+
+        def load_x(b, first, count):
             nc.sync.dma_start(
-                out=x_sb[:, 2 * chunk : 2 * chunk + 2, :].rearrange("p j c -> p (j c)"),
-                in_=x_view[:, :, 2 * C * chunk : 2 * C * (chunk + 1)],
+                out=x_sb[:, TOKENS * b + first : TOKENS * b + first + count, :].rearrange("p j c -> p (j c)"),
+                in_=x_view[b][:, C * first : C * (first + count)],
             )
-        nc.scalar.dma_start(out=rows[0:1, 0:C], in_=q_bias.rearrange("(o n) -> o n", o=1))
-        nc.scalar.dma_start(out=rows[0:1, C : 2 * C], in_=v_bias.rearrange("(o n) -> o n", o=1))
-        nc.scalar.dma_start(
-            out=rows[0:1, 2 * C : 2 * C + H],
-            in_=log_scale_mul.rearrange("a h b c -> a (h b c)"),
-        )
-        for r in range(4):
-            nc.sync.dma_start(
-                out=w_planes[r:P:32, :, :].bitcast(I32),
-                in_=W_qkv_scales[:, r:16:4, :].rearrange("g q n -> q g n").bitcast(I32),
-            )
-        w_words = keep.tile([P, PASSES, 2 * 3 * C], U8, align_bytes=64)
+
+        w_words = {}
         w_view = W_qkv_words.rearrange("g p n -> p g n")
-        for half in range(2):
-            for tensor in range(3):
-                first = 2 * (C * tensor + (C // 2) * half)
+
+        def load_w(tensor, half):
+            first = 2 * (C * tensor + (C // 2) * half)
+            piece = keep.tile([P, PASSES, C], U8, align_bytes=64, name="w_words_%d_%d" % (tensor, half))
+            nc.sync.dma_start(out=piece[:].bitcast(I32), in_=w_view[:, :, first : first + C].bitcast(I32))
+            w_words[(tensor, half)] = piece
+
+        logs = keep.tile([P, H], BF16)
+        with tc.manual_schedule(engines={mybir.EngineType.SP}):
+            nc.sync.dma_start(out=logs[:], in_=log_scale_mul.rearrange("a h b c -> (a h b c)").partition_broadcast(P))
+            load_x(0, 0, 1)
+            load_x(0, 1, 1)
+            nc.sync.dma_start(out=rows[0:1, 0:C], in_=q_bias.rearrange("(o n) -> o n", o=1))
+            nc.sync.dma_start(out=rows[0:1, C : 2 * C], in_=v_bias.rearrange("(o n) -> o n", o=1))
+            load_x(0, 2, 1)
+            load_x(0, 3, 1)
+            for r in range(4):
                 nc.sync.dma_start(
-                    out=w_words[:, :, first : first + C].bitcast(I32),
-                    in_=w_view[:, :, first : first + C].bitcast(I32),
+                    out=w_planes[r:P:32, :, :].bitcast(I32),
+                    in_=W_qkv_scales[:, r:16:4, :].rearrange("g q n -> q g n").bitcast(I32),
                 )
+            load_w(K, 0)
+            load_w(Q, 0)
+            load_w(V, 0)
+            load_x(1, 0, 2)
+            load_x(1, 2, 2)
+            load_w(K, 1)
+            load_w(Q, 1)
+            load_w(V, 1)
+        raised = keep.tile([P, H], F32)
+        nc.scalar.activation(out=raised[:], in_=logs[:], func=ACT.Exp)
+        nc.scalar.activation(out=warm[:, 2:3], in_=raised[:, 0:1], func=ACT.Abs_reciprocal_sqrt)
 
         x_words = x_sb[:].bitcast(F32)
-        x_codes = keep.tile([P, TOKENS_PER_PARTITION, PASSES, P], U32, align_bytes=64)
-        x_planes = keep.tile([P, TOKENS_PER_PARTITION, PASSES, P], U8, align_bytes=64)
-        for chunk in range(4):
-            grouped = regroup.tile([P, 2, 2 * K_PASS], BF16, align_bytes=64)
-            for jj in range(2):
-                j = 2 * chunk + jj
-                flipped = psum.tile([P, PASSES, 2, P], F32, tag=("brief" if jj == 0 else "held"))
-                for g in range(PASSES):
-                    for u in range(2):
-                        nc.tensor.transpose(
-                            flipped[:, g, u, :],
-                            x_words[:, j, 256 * g + u : 256 * (g + 1) : 2],
-                            ident[:],
-                        )
-                target = grouped[:, jj, :].bitcast(F32).rearrange(
-                    "p (g m u) -> p g m u", g=PASSES, u=2
-                )
-                source = flipped[:].rearrange("p g u m -> p g m u")
-                if jj == 0:
-                    nc.vector.tensor_copy(out=target, in_=source)
-                else:
-                    nc.scalar.copy(out=target, in_=source)
+        x_codes = keep.tile([P, TILES, PASSES, P], U32, align_bytes=64)
+        x_planes = keep.tile([P, TILES, PASSES, P], U8, align_bytes=64)
+
+        def flip(t):
+            flipped = psum.tile([P, PASSES, 2, P], F32, tag="brief", name="flipped")
+            for g in range(PASSES):
+                for u in range(2):
+                    nc.tensor.transpose(flipped[:, g, u, :], x_words[:, t, 256 * g + u : 256 * (g + 1) : 2], ident[:])
+            return flipped
+
+        def regroup_x(flipped, on_vector):
+            grouped = regroup.tile([P, 2 * K_PASS], BF16, align_bytes=64, name="grouped")
+            target = grouped[:].bitcast(F32).rearrange("p (g m u) -> p g m u", g=PASSES, u=2)
+            source = flipped[:].rearrange("p g u m -> p g m u")
+            if on_vector:
+                nc.vector.tensor_copy(out=target, in_=source)
+            else:
+                nc.scalar.copy(out=target, in_=source)
+            return grouped
+
+        def quantise(t, grouped):
             nc.vector.quantize_mx(
-                out=x_codes[:, 2 * chunk : 2 * chunk + 2, :, :]
-                .rearrange("p j g m -> p (j g m)")
-                .bitcast(FP8X4),
-                scales=x_planes[:, 2 * chunk : 2 * chunk + 2, :, :].rearrange("p j g m -> p (j g m)"),
-                in_=grouped[:].rearrange("p j c -> p (j c)"),
+                out=x_codes[:, t, :, :].rearrange("p g m -> p (g m)").bitcast(FP8X4),
+                scales=x_planes[:, t, :, :].rearrange("p g m -> p (g m)"),
+                in_=grouped[:],
             )
 
         bias_sb = keep.tile([P, 2 * C], F32)
-        for piece in range(4):
-            spread = psum.tile([P, 512], F32, tag="brief")
-            nc.tensor.matmul(
-                spread[:], lhsT=ones[:], rhs=rows[:, 512 * piece : 512 * (piece + 1)],
-                start=True, stop=True,
+
+        def spread_bias(piece):
+            spread = psum.tile([P, BANK], F32, tag="brief", name="spread")
+            nc.tensor.matmul(spread[:], lhsT=ones[:], rhs=rows[:, BANK * piece : BANK * (piece + 1)], start=True, stop=True)
+            return spread
+
+        def keep_bias(piece, spread, on_vector):
+            if on_vector:
+                nc.vector.tensor_copy(out=bias_sb[:, BANK * piece : BANK * (piece + 1)], in_=spread[:])
+            else:
+                nc.scalar.copy(out=bias_sb[:, BANK * piece : BANK * (piece + 1)], in_=spread[:])
+
+
+        def project(tensor, i):
+            b, pair = i // PAIRS, i % PAIRS
+            if tensor == K:
+                bank = psum_k.tile([P, TOKENS, PAIR], F32, tag="held", name="bank")
+            else:
+                bank = psum.tile([P, TOKENS, PAIR], F32, tag="brief", name="bank")
+            col = C * tensor + PAIR * pair
+            piece = w_words[(tensor, pair // (PAIRS // 2))]
+            inside = 2 * PAIR * (pair % (PAIRS // 2))
+            for j in range(TOKENS):
+                t = TOKENS * b + j
+                for g in range(PASSES):
+                    nc.tensor.matmul_mx(
+                        out=bank[:, j, :],
+                        lhsT=x_codes[:, t, g, :].bitcast(FP8X4),
+                        lhsT_scale=x_planes[:, t, g, :],
+                        rhs=piece[:, g, inside : inside + 2 * PAIR].bitcast(FP4X4),
+                        rhs_scale=w_planes[:, g, col : col + PAIR],
+                        start=(g == 0),
+                        stop=(g == PASSES - 1),
+                    )
+            return bank
+
+        def in_bank_order(result):
+            return result[:].rearrange("p h j d -> p j h d")
+
+        def by_head(bank):
+            return bank[:].rearrange("p j (h d) -> p j h d", h=2)
+
+        def add_bias(bank, result, first):
+            nc.vector.tensor_tensor(
+                out=in_bank_order(result),
+                in0=by_head(bank),
+                in1=bias_sb[:, first : first + PAIR].rearrange("p (h d) -> p h d", h=2).unsqueeze(1).to_broadcast([P, TOKENS, 2, D]),
+                op=ALU.add,
             )
-            nc.scalar.copy(out=bias_sb[:, 512 * piece : 512 * (piece + 1)], in_=spread[:])
-        spread = psum.tile([P, 512], F32, tag="held")
-        nc.tensor.matmul(
-            spread[:, 0:D], lhsT=ones[:], rhs=rows[:, 2 * C : 2 * C + D], start=True, stop=True
-        )
-        scale_raw = keep.tile([P, H], F32)
-        nc.scalar.activation(out=scale_raw[:], in_=spread[:, 0:H], func=ACT.Exp)
-        scale_mul = keep.tile([P, H], F32)
-        nc.vector.tensor_scalar_min(out=scale_mul[:], in0=scale_raw[:], scalar1=MAX_SCALE)
 
-        def project(first_column, tag):
-            banks = []
-            for half in range(HALVES):
-                bank = psum.tile([P, BANK_TILES, PAIR], F32, tag=tag, name="bank")
-                for jj in range(BANK_TILES):
-                    j = BANK_TILES * half + jj
-                    for g in range(PASSES):
-                        nc.tensor.matmul_mx(
-                            out=bank[:, jj, :],
-                            lhsT=x_codes[:, j, g, :].bitcast(FP8X4),
-                            lhsT_scale=x_planes[:, j, g, :],
-                            rhs=w_words[:, g, 2 * first_column : 2 * (first_column + PAIR)].bitcast(FP4X4),
-                            rhs_scale=w_planes[:, g, first_column : first_column + PAIR],
-                            start=(g == 0),
-                            stop=(g == PASSES - 1),
-                        )
-                banks.append(bank)
-            return banks
-
-        def by_token_tile(result, half):
-            return result[:, :, BANK_TILES * half : BANK_TILES * (half + 1), :].rearrange(
-                "p h j d -> p j h d"
-            )
-
-        def add_bias(banks, bias_columns):
-            result = stage.tile([P, 2, TOKENS_PER_PARTITION, D], F32, tag="result", name="result")
-            for half in range(HALVES):
-                nc.vector.tensor_tensor(
-                    out=by_token_tile(result, half),
-                    in0=banks[half][:].rearrange("p j (h d) -> p j h d", h=2),
-                    in1=bias_columns.rearrange("p (h d) -> p h d", h=2)
-                    .unsqueeze(1)
-                    .to_broadcast([P, BANK_TILES, 2, D]),
-                    op=ALU.add,
-                )
-            return result
-
-        def inverse_norms(head_of):
-            squares = small.tile([P, 2, TOKENS_PER_PARTITION], F32, tag="squares", name="squares")
-            for j in range(TOKENS_PER_PARTITION):
+        def squares_narrow(vector_of, sums, first):
+            for j in range(TOKENS):
                 for h in range(2):
                     unused = small.tile([P, D], BF16, tag="unused", name="unused")
-                    nc.scalar.activation(
-                        out=unused[:], in_=head_of(h, j), func=ACT.Square,
-                        accum_out=squares[:, h, j : j + 1],
-                    )
-            excess = small.tile([P, 2, TOKENS_PER_PARTITION], F32, tag="excess", name="excess")
-            nc.scalar.activation(out=excess[:], in_=squares[:], func=ACT.Relu, bias=-EPS_SQUARED)
-            inverse = small.tile([P, 2, TOKENS_PER_PARTITION], F32, tag="inverse", name="inverse")
-            nc.scalar.activation(
-                out=inverse[:], in_=excess[:], func=ACT.Abs_reciprocal_sqrt, bias=EPS_SQUARED
-            )
-            return inverse
+                    nc.scalar.activation(out=unused[:], in_=vector_of(j, h), func=ACT.Square, accum_out=sums[:, first + 2 * j + h : first + 2 * j + h + 1])
 
-        def store(out, pair, result):
-            view = out.rearrange("b h (p j) d -> h p b (j d)", j=TOKENS_PER_PARTITION)
-            for h in range(2):
-                nc.sync.dma_start(
-                    out=view[2 * pair + h], in_=result[:, h, :, :].rearrange("p j d -> p (j d)")
-                )
+        def squares_wide(bank):
+            squared = scratch.tile([P, SUMS, D], F32, tag="squared", name="squared")
+            nc.scalar.activation(out=squared[:].rearrange("p s d -> p (s d)"), in_=bank[:].rearrange("p j n -> p (j n)"), func=ACT.Square)
+            return squared
 
-        def front(pair):
-            q_raw = add_bias(project(PAIR * pair, "brief"), bias_sb[:, PAIR * pair : PAIR * (pair + 1)])
-            k_banks = project(C + PAIR * pair, "held")
-            v = add_bias(
-                project(2 * C + PAIR * pair, "brief"), bias_sb[:, C + PAIR * pair : C + PAIR * (pair + 1)]
-            )
-            store(out_2, pair, v)
-            q_inverse = inverse_norms(lambda h, j: q_raw[:, h, j, :])
-            k_inverse = inverse_norms(
-                lambda h, j: k_banks[j // BANK_TILES][:, j % BANK_TILES, D * h : D * (h + 1)]
-            )
-            return q_raw, q_inverse, k_banks, k_inverse
-
-        def back(pair, q_raw, q_inverse, k_banks, k_inverse):
-            q_factor = small.tile([P, 2, TOKENS_PER_PARTITION], F32, tag="q_factor", name="q_factor")
+        def fold_wide(squared):
             nc.gpsimd.tensor_tensor(
-                out=q_factor[:], in0=q_inverse[:],
-                in1=scale_mul[:, 2 * pair : 2 * pair + 2].unsqueeze(2).to_broadcast([P, 2, TOKENS_PER_PARTITION]),
+                out=squared[:, :, 0 : D // 2], in0=squared[:, :, 0 : D // 2], in1=squared[:, :, D // 2 : D], op=ALU.add
+            )
+
+        def reduce_wide(squared, sums, width):
+            nc.vector.tensor_reduce(out=sums[:, 0:SUMS], in_=squared[:, :, 0:width], axis=AX.X, op=ALU.add)
+
+        def inverse_root(sums, inverse):
+            nc.scalar.activation(out=inverse[:], in_=sums[:], func=ACT.Abs_reciprocal_sqrt, bias=TINY)
+
+        def factors(inverse, factor, pair):
+            nc.vector.scalar_tensor_tensor(
+                out=factor[:], in0=inverse[:], scalar=INV_EPS, in1=multiplier[:, pair, :], op0=ALU.min, op1=ALU.mult
+            )
+
+        def scale_k(bank, factor, result):
+            nc.vector.tensor_tensor(
+                out=in_bank_order(result),
+                in0=by_head(bank),
+                in1=factor[:, 0:SUMS].rearrange("p (j h) -> p j h", h=2).unsqueeze(3).to_broadcast([P, TOKENS, 2, D]),
                 op=ALU.mult,
             )
-            for h in range(2):
-                nc.gpsimd.tensor_tensor(
-                    out=q_raw[:, h, :, :], in0=q_raw[:, h, :, :],
-                    in1=q_factor[:, h, :].unsqueeze(2).to_broadcast([P, TOKENS_PER_PARTITION, D]),
-                    op=ALU.mult,
-                )
-            k = stage.tile([P, 2, TOKENS_PER_PARTITION, D], F32, tag="result", name="k")
-            for half in range(HALVES):
-                nc.vector.tensor_tensor(
-                    out=by_token_tile(k, half),
-                    in0=k_banks[half][:].rearrange("p j (h d) -> p j h d", h=2),
-                    in1=k_inverse[:, :, BANK_TILES * half : BANK_TILES * (half + 1)]
-                    .rearrange("p h j -> p j h")
-                    .unsqueeze(3)
-                    .to_broadcast([P, BANK_TILES, 2, D]),
-                    op=ALU.mult,
-                )
-            store(out_1, pair, k)
-            store(out_0, pair, q_raw)
 
-        waiting = None
-        for pair in range(HEAD_PAIRS):
-            fresh = front(pair)
-            if waiting is not None:
-                back(pair - 1, *waiting)
-            waiting = fresh
-        back(HEAD_PAIRS - 1, *waiting)
+        def scale_q(result, factor):
+            nc.gpsimd.tensor_tensor(
+                out=result[:],
+                in0=result[:],
+                in1=factor[:, SUMS : 2 * SUMS].rearrange("p (j h) -> p h j", h=2).unsqueeze(3).to_broadcast([P, 2, TOKENS, D]),
+                op=ALU.mult,
+            )
+
+        def store(tensor, i, result):
+            b, pair = i // PAIRS, i % PAIRS
+            view = outs[tensor].rearrange("b h (p j) d -> b p h (j d)", j=TOKENS)
+            nc.sync.dma_start(out=view[b][:, 2 * pair : 2 * pair + 2, :], in_=result[:].rearrange("p h j d -> p h (j d)"))
+
+        def new_small(tag):
+            t = small.tile([P, 2 * SUMS], F32, tag=tag, name=tag)
+            return t
+
+        grouped = [None] * TILES
+        flipped = [None] * TILES
+        lead = max(LEAD_K, LEAD_Q, LEAD_V)
+        first_step = -lead
+        last_step = UNITS - 1 - min(LEAD_K, LEAD_Q, LEAD_V) + 3
+        banks, res, sm, sq = {}, {}, {}, {}
+
+        def ok(i):
+            return 0 <= i < UNITS
+
+        def fill(tensor, i):
+            if ok(i):
+                banks[(tensor, i)] = project(tensor, i)
+                result = stage.tile([P, 2, TOKENS, D], F32, tag="result", name="result")
+                res[(tensor, i)] = result
+
+        def fills(s):
+            fill(K, s + LEAD_K)
+            fill(Q, s + LEAD_Q)
+            fill(V, s + LEAD_V)
+
+        for t in range(TOKENS):
+            flipped[t] = flip(t)
+            grouped[t] = regroup_x(flipped[t], t in VEC_COPY)
+            if t == 0:
+                quantise(0, grouped[0])
+            if t == 2:
+                quantise(1, grouped[1])
+                quantise(2, grouped[2])
+        quantise(3, grouped[3])
+        nc.vector.tensor_scalar_min(
+            out=multiplier[:, :, SUMS : 2 * SUMS].rearrange("p r (j h) -> p r j h", h=2),
+            in0=raised[:].rearrange("p (r h) -> p r h", h=2).unsqueeze(2).to_broadcast([P, PAIRS, TOKENS, 2]),
+            scalar1=MAX_SCALE,
+        )
+        spreads = [spread_bias(0), spread_bias(2)]
+        keep_bias(0, spreads[0], False)
+        keep_bias(2, spreads[1], False)
+        fills(first_step)
+
+        for s in range(first_step, last_step + 1):
+            ik, iq, iv = s + LEAD_K, s + LEAD_Q, s + LEAD_V
+            u = s + lead
+            i = ik
+            assert LEAD_K == LEAD_Q
+            if ok(i):
+                sm[("s", i)] = new_small("sums")
+                if i % PAIRS in NARROW_K:
+                    squares_narrow(lambda j, h: banks[(K, i)][:, j, D * h : D * (h + 1)], sm[("s", i)], 0)
+                else:
+                    sq[i] = squares_wide(banks[(K, i)])
+                    if FOLD and i < NO_FOLD_FROM:
+                        fold_wide(sq[i])
+                add_bias(banks[(Q, i)], res[(Q, i)], PAIR * (i % PAIRS))
+            if ok(iv):
+                add_bias(banks[(V, iv)], res[(V, iv)], C + PAIR * (iv % PAIRS))
+                store(V, iv, res[(V, iv)])
+            fills(s + 1)
+            if u in FLIP_AT:
+                flipped[FLIP_AT[u]] = flip(FLIP_AT[u])
+            extra = None
+            if u == 1:
+                extra = spread_bias(1)
+            if u == 2:
+                extra = spread_bias(3)
+            if u - 1 in FLIP_AT:
+                quantise(FLIP_AT[u - 1], grouped[FLIP_AT[u - 1]])
+            if ok(i - 1):
+                sm[("i", i - 1)] = new_small("inverse")
+                sm[("f", i - 1)] = new_small("factor")
+                inverse_root(sm[("s", i - 1)], sm[("i", i - 1)])
+                factors(sm[("i", i - 1)], sm[("f", i - 1)], (i - 1) % PAIRS)
+                scale_k(banks[(K, i - 1)], sm[("f", i - 1)], res[(K, i - 1)])
+                store(K, i - 1, res[(K, i - 1)])
+                scale_q(res[(Q, i - 1)], sm[("f", i - 1)])
+                store(Q, i - 1, res[(Q, i - 1)])
+            if ok(i):
+                squares_narrow(lambda j, h: res[(Q, i)][:, h, j, :], sm[("s", i)], SUMS)
+            if u in FLIP_AT:
+                grouped[FLIP_AT[u]] = regroup_x(flipped[FLIP_AT[u]], False)
+            if u == 1:
+                keep_bias(1, extra, False)
+            if u == 2:
+                keep_bias(3, extra, False)
+            if ok(i) and i % PAIRS not in NARROW_K:
+                reduce_wide(sq[i], sm[("s", i)], D // 2 if (FOLD and i < NO_FOLD_FROM) else D)

@@ -25,15 +25,16 @@ BANK = TOKENS * PAIR
 SUMS = 2 * TOKENS
 Q, K, V = 0, 1, 2
 MAX_SCALE = 100.0
-INV_EPS = 1.0e12
-TINY = 1.0e-30
+EPS_SQUARED = 1.0e-24
 
 NARROW_K = ()
 FOLD = True
 LEAD_K, LEAD_Q, LEAD_V = 0, 0, -1
+VECTOR_Q_FROM = 16
 NO_FOLD_FROM = 15
 LATER_BIAS = {}
-FLIP_AT = {2: 4, 3: 5, 4: 6, 5: 7}
+FLIP_AT = {1: 4, 2: 5, 3: 6, 4: 7}
+QUANT_AT = 5
 VEC_COPY = (0, 2)
 
 FLOPS = 2 * B * L * C * 3 * C
@@ -60,8 +61,6 @@ def tile_selfattention_pa_kernel(
         nc.vector.memset(ones[:], 1.0)
         ident = keep.tile([P, P], F32)
         make_identity(nc, ident[:])
-        multiplier = keep.tile([P, PAIRS, 2 * SUMS], F32)
-        nc.gpsimd.memset(multiplier[:], 1.0)
 
         x_sb = keep.tile([P, TILES, C], BF16)
         x_view = x.rearrange("b (p j) c -> b p (j c)", j=TOKENS)
@@ -104,7 +103,7 @@ def tile_selfattention_pa_kernel(
             load_w(Q, 1)
             load_w(V, 1)
         raised = keep.tile([P, H], F32)
-        nc.scalar.activation(out=raised[:], in_=logs[:], func=ACT.Exp)
+        nc.scalar.activation(out=raised[:], in_=logs[:], func=ACT.Exp, scale=-2.0)
         nc.scalar.activation(out=warm[:, 2:3], in_=raised[:, 0:1], func=ACT.Abs_reciprocal_sqrt)
 
         x_words = x_sb[:].bitcast(F32)
@@ -118,21 +117,19 @@ def tile_selfattention_pa_kernel(
                     nc.tensor.transpose(flipped[:, g, u, :], x_words[:, t, 256 * g + u : 256 * (g + 1) : 2], ident[:])
             return flipped
 
-        def regroup_x(flipped, on_vector):
-            grouped = regroup.tile([P, 2 * K_PASS], BF16, align_bytes=64, name="grouped")
-            target = grouped[:].bitcast(F32).rearrange("p (g m u) -> p g m u", g=PASSES, u=2)
+        def regroup_x(flipped, grouped, on_vector):
+            target = grouped.bitcast(F32).rearrange("p (g m u) -> p g m u", g=PASSES, u=2)
             source = flipped[:].rearrange("p g u m -> p g m u")
             if on_vector:
                 nc.vector.tensor_copy(out=target, in_=source)
             else:
                 nc.scalar.copy(out=target, in_=source)
-            return grouped
 
-        def quantise(t, grouped):
+        def quantise(t, count, grouped):
             nc.vector.quantize_mx(
-                out=x_codes[:, t, :, :].rearrange("p g m -> p (g m)").bitcast(FP8X4),
-                scales=x_planes[:, t, :, :].rearrange("p g m -> p (g m)"),
-                in_=grouped[:],
+                out=x_codes[:, t : t + count, :, :].rearrange("p t g m -> p (t g m)").bitcast(FP8X4),
+                scales=x_planes[:, t : t + count, :, :].rearrange("p t g m -> p (t g m)"),
+                in_=grouped,
             )
 
         bias_sb = keep.tile([P, 2 * C], F32)
@@ -186,8 +183,8 @@ def tile_selfattention_pa_kernel(
                 op=ALU.add,
             )
 
-        def squares_narrow(vector_of, sums, first):
-            for j in range(TOKENS):
+        def squares_narrow(vector_of, sums, first, tokens):
+            for j in tokens:
                 for h in range(2):
                     unused = small.tile([P, D], BF16, tag="unused", name="unused")
                     nc.scalar.activation(out=unused[:], in_=vector_of(j, h), func=ACT.Square, accum_out=sums[:, first + 2 * j + h : first + 2 * j + h + 1])
@@ -205,13 +202,19 @@ def tile_selfattention_pa_kernel(
         def reduce_wide(squared, sums, width):
             nc.vector.tensor_reduce(out=sums[:, 0:SUMS], in_=squared[:, :, 0:width], axis=AX.X, op=ALU.add)
 
-        def inverse_root(sums, inverse):
-            nc.scalar.activation(out=inverse[:], in_=sums[:], func=ACT.Abs_reciprocal_sqrt, bias=TINY)
+        def excess_over_eps(sums, excess, lo, hi):
+            nc.scalar.activation(out=excess[:, lo:hi], in_=sums[:, lo:hi], func=ACT.Relu, bias=-EPS_SQUARED)
 
-        def factors(inverse, factor, pair):
-            nc.vector.scalar_tensor_tensor(
-                out=factor[:], in0=inverse[:], scalar=INV_EPS, in1=multiplier[:, pair, :], op0=ALU.min, op1=ALU.mult
-            )
+        def k_factors(excess, factor):
+            nc.scalar.activation(out=factor[:, 0:SUMS], in_=excess[:, 0:SUMS], func=ACT.Abs_reciprocal_sqrt, bias=EPS_SQUARED)
+
+        def q_factors(excess, factor, pair):
+            for h in range(2):
+                head = 2 * pair + h
+                nc.scalar.activation(
+                    out=factor[:, SUMS + h : 2 * SUMS : 2], in_=excess[:, SUMS + h : 2 * SUMS : 2], func=ACT.Abs_reciprocal_sqrt,
+                    scale=shrink[:, head : head + 1], bias=shrunk_eps[:, head : head + 1],
+                )
 
         def scale_k(bank, factor, result):
             nc.vector.tensor_tensor(
@@ -221,8 +224,9 @@ def tile_selfattention_pa_kernel(
                 op=ALU.mult,
             )
 
-        def scale_q(result, factor):
-            nc.gpsimd.tensor_tensor(
+        def scale_q(result, factor, on_vector):
+            engine = nc.vector if on_vector else nc.gpsimd
+            engine.tensor_tensor(
                 out=result[:],
                 in0=result[:],
                 in1=factor[:, SUMS : 2 * SUMS].rearrange("p (j h) -> p h j", h=2).unsqueeze(3).to_broadcast([P, 2, TOKENS, D]),
@@ -238,7 +242,6 @@ def tile_selfattention_pa_kernel(
             t = small.tile([P, 2 * SUMS], F32, tag=tag, name=tag)
             return t
 
-        grouped = [None] * TILES
         flipped = [None] * TILES
         lead = max(LEAD_K, LEAD_Q, LEAD_V)
         first_step = -lead
@@ -259,39 +262,51 @@ def tile_selfattention_pa_kernel(
             fill(Q, s + LEAD_Q)
             fill(V, s + LEAD_V)
 
+        grouped = keep.tile([P, TILES, 2 * K_PASS], BF16, align_bytes=64)
         for t in range(TOKENS):
             flipped[t] = flip(t)
-            grouped[t] = regroup_x(flipped[t], t in VEC_COPY)
+            regroup_x(flipped[t], grouped[:, t, :], t in VEC_COPY)
             if t == 0:
-                quantise(0, grouped[0])
+                quantise(0, 1, grouped[:, 0, :])
             if t == 2:
-                quantise(1, grouped[1])
-                quantise(2, grouped[2])
-        quantise(3, grouped[3])
-        nc.vector.tensor_scalar_min(
-            out=multiplier[:, :, SUMS : 2 * SUMS].rearrange("p r (j h) -> p r j h", h=2),
-            in0=raised[:].rearrange("p (r h) -> p r h", h=2).unsqueeze(2).to_broadcast([P, PAIRS, TOKENS, 2]),
-            scalar1=MAX_SCALE,
+                quantise(1, 1, grouped[:, 1, :])
+                quantise(2, 1, grouped[:, 2, :])
+        quantise(3, 1, grouped[:, 3, :])
+        shrink = keep.tile([P, H], F32)
+        nc.vector.tensor_scalar_max(out=shrink[:], in0=raised[:], scalar1=1.0 / (MAX_SCALE * MAX_SCALE))
+        shrunk_eps = keep.tile([P, H], F32)
+        nc.vector.tensor_scalar(
+            out=shrunk_eps[:], in0=raised[:], scalar1=1.0 / (MAX_SCALE * MAX_SCALE), scalar2=EPS_SQUARED, op0=ALU.max, op1=ALU.mult
         )
         spreads = [spread_bias(0), spread_bias(2)]
         keep_bias(0, spreads[0], False)
         keep_bias(2, spreads[1], False)
         fills(first_step)
 
+        def part(ik, iq):
+            return (0 if ok(ik) else SUMS), (2 * SUMS if ok(iq) else SUMS)
+
         for s in range(first_step, last_step + 1):
             ik, iq, iv = s + LEAD_K, s + LEAD_Q, s + LEAD_V
             u = s + lead
-            i = ik
-            assert LEAD_K == LEAD_Q
-            if ok(i):
-                sm[("s", i)] = new_small("sums")
-                if i % PAIRS in NARROW_K:
-                    squares_narrow(lambda j, h: banks[(K, i)][:, j, D * h : D * (h + 1)], sm[("s", i)], 0)
+            if ok(ik) or ok(iq):
+                sm[("s", s)] = new_small("sums")
+            if ok(ik - 1) or ok(iq - 1):
+                lo, hi = part(ik - 1, iq - 1)
+                sm[("e", s - 1)] = new_small("excess")
+                sm[("f", s - 1)] = new_small("factor")
+                excess_over_eps(sm[("s", s - 1)], sm[("e", s - 1)], lo, hi)
+            if ok(ik):
+                if ik % PAIRS in NARROW_K:
+                    squares_narrow(lambda j, h: banks[(K, ik)][:, j, D * h : D * (h + 1)], sm[("s", s)], 0, range(TOKENS))
                 else:
-                    sq[i] = squares_wide(banks[(K, i)])
-                    if FOLD and i < NO_FOLD_FROM:
-                        fold_wide(sq[i])
-                add_bias(banks[(Q, i)], res[(Q, i)], PAIR * (i % PAIRS))
+                    sq[ik] = squares_wide(banks[(K, ik)])
+                    if FOLD and ik < NO_FOLD_FROM:
+                        fold_wide(sq[ik])
+            if ok(iq):
+                add_bias(banks[(Q, iq)], res[(Q, iq)], PAIR * (iq % PAIRS))
+            if ok(ik) and ik >= NO_FOLD_FROM and ik % PAIRS not in NARROW_K:
+                reduce_wide(sq[ik], sm[("s", s)], D)
             if ok(iv):
                 add_bias(banks[(V, iv)], res[(V, iv)], C + PAIR * (iv % PAIRS))
                 store(V, iv, res[(V, iv)])
@@ -303,24 +318,23 @@ def tile_selfattention_pa_kernel(
                 extra = spread_bias(1)
             if u == 2:
                 extra = spread_bias(3)
-            if u - 1 in FLIP_AT:
-                quantise(FLIP_AT[u - 1], grouped[FLIP_AT[u - 1]])
-            if ok(i - 1):
-                sm[("i", i - 1)] = new_small("inverse")
-                sm[("f", i - 1)] = new_small("factor")
-                inverse_root(sm[("s", i - 1)], sm[("i", i - 1)])
-                factors(sm[("i", i - 1)], sm[("f", i - 1)], (i - 1) % PAIRS)
-                scale_k(banks[(K, i - 1)], sm[("f", i - 1)], res[(K, i - 1)])
-                store(K, i - 1, res[(K, i - 1)])
-                scale_q(res[(Q, i - 1)], sm[("f", i - 1)])
-                store(Q, i - 1, res[(Q, i - 1)])
-            if ok(i):
-                squares_narrow(lambda j, h: res[(Q, i)][:, h, j, :], sm[("s", i)], SUMS)
+            if u == QUANT_AT:
+                quantise(TOKENS, TOKENS, grouped[:, TOKENS:TILES, :].rearrange("p t c -> p (t c)"))
+            if ok(ik - 1):
+                k_factors(sm[("e", s - 1)], sm[("f", s - 1)])
+                scale_k(banks[(K, ik - 1)], sm[("f", s - 1)], res[(K, ik - 1)])
+                store(K, ik - 1, res[(K, ik - 1)])
+            if ok(iq - 1):
+                q_factors(sm[("e", s - 1)], sm[("f", s - 1)], (iq - 1) % PAIRS)
+                scale_q(res[(Q, iq - 1)], sm[("f", s - 1)], iq - 1 >= VECTOR_Q_FROM)
+                store(Q, iq - 1, res[(Q, iq - 1)])
+            if ok(iq):
+                squares_narrow(lambda j, h: res[(Q, iq)][:, h, j, :], sm[("s", s)], SUMS, range(TOKENS))
             if u in FLIP_AT:
-                grouped[FLIP_AT[u]] = regroup_x(flipped[FLIP_AT[u]], False)
+                regroup_x(flipped[FLIP_AT[u]], grouped[:, FLIP_AT[u], :], False)
             if u == 1:
                 keep_bias(1, extra, False)
             if u == 2:
                 keep_bias(3, extra, False)
-            if ok(i) and i % PAIRS not in NARROW_K:
-                reduce_wide(sq[i], sm[("s", i)], D // 2 if (FOLD and i < NO_FOLD_FROM) else D)
+            if ok(ik) and ik < NO_FOLD_FROM and ik % PAIRS not in NARROW_K:
+                reduce_wide(sq[ik], sm[("s", s)], D // 2 if FOLD else D)

@@ -16,11 +16,12 @@ P = 128
 B, L, C, H, D = 2, 512, 1024, 16, 64
 K_PASS = 512
 PASSES = C // K_PASS
-TOKENS = L // P
-TILES = B * TOKENS
+TILES = B * L // P
+TOKENS = 4
+HALVES = TILES // TOKENS
 PAIR = 2 * D
 PAIRS = H // 2
-UNITS = B * PAIRS
+UNITS = HALVES * PAIRS
 BANK = TOKENS * PAIR
 SUMS = 2 * TOKENS
 Q, K, V = 0, 1, 2
@@ -29,13 +30,11 @@ EPS_SQUARED = 1.0e-24
 
 NARROW_K = ()
 FOLD = True
-LEAD_K, LEAD_Q, LEAD_V = 0, 0, -1
+LEAD_V = 1
 VECTOR_Q_FROM = 16
 NO_FOLD_FROM = 15
 LATER_BIAS = {}
-FLIP_AT = {1: 4, 2: 5, 3: 6, 4: 7}
-QUANT_AT = 5
-VEC_COPY = (0, 2)
+VEC_COPY = (0, 2, 4, 6)
 
 FLOPS = 2 * B * L * C * 3 * C
 
@@ -63,12 +62,12 @@ def tile_selfattention_pa_kernel(
         make_identity(nc, ident[:])
 
         x_sb = keep.tile([P, TILES, C], BF16)
-        x_view = x.rearrange("b (p j) c -> b p (j c)", j=TOKENS)
+        x_view = x.rearrange("b (p j) c -> p b (j c)", j=TILES)
 
-        def load_x(b, first, count):
+        def load_x(first, count):
             nc.sync.dma_start(
-                out=x_sb[:, TOKENS * b + first : TOKENS * b + first + count, :].rearrange("p j c -> p (j c)"),
-                in_=x_view[b][:, C * first : C * (first + count)],
+                out=x_sb[:, first : first + count, :].rearrange("p j c -> p (j c)"),
+                in_=x_view[:, :, C * first : C * (first + count)],
             )
 
         w_words = {}
@@ -83,25 +82,21 @@ def tile_selfattention_pa_kernel(
         logs = keep.tile([P, H], BF16)
         with tc.manual_schedule(engines={mybir.EngineType.SP}):
             nc.sync.dma_start(out=logs[:], in_=log_scale_mul.rearrange("a h b c -> (a h b c)").partition_broadcast(P))
-            load_x(0, 0, 1)
-            load_x(0, 1, 1)
+            load_x(0, 1)
+            load_x(1, 1)
             nc.sync.dma_start(out=rows[0:1, 0:C], in_=q_bias.rearrange("(o n) -> o n", o=1))
             nc.sync.dma_start(out=rows[0:1, C : 2 * C], in_=v_bias.rearrange("(o n) -> o n", o=1))
-            load_x(0, 2, 1)
-            load_x(0, 3, 1)
+            load_x(2, 2)
+            load_x(4, 2)
+            load_x(6, 2)
             for r in range(4):
                 nc.sync.dma_start(
                     out=w_planes[r:P:32, :, :].bitcast(I32),
                     in_=W_qkv_scales[:, r:16:4, :].rearrange("g q n -> q g n").bitcast(I32),
                 )
-            load_w(K, 0)
-            load_w(Q, 0)
-            load_w(V, 0)
-            load_x(1, 0, 2)
-            load_x(1, 2, 2)
-            load_w(K, 1)
-            load_w(Q, 1)
-            load_w(V, 1)
+            for half in range(2):
+                for tensor in (V, K, Q):
+                    load_w(tensor, half)
         raised = keep.tile([P, H], F32)
         nc.scalar.activation(out=raised[:], in_=logs[:], func=ACT.Exp, scale=-2.0)
         nc.scalar.activation(out=warm[:, 2:3], in_=raised[:, 0:1], func=ACT.Abs_reciprocal_sqrt)
@@ -147,7 +142,7 @@ def tile_selfattention_pa_kernel(
 
 
         def project(tensor, i):
-            b, pair = i // PAIRS, i % PAIRS
+            pair, half = i // HALVES, i % HALVES
             if tensor == K:
                 bank = psum_k.tile([P, TOKENS, PAIR], F32, tag="held", name="bank")
             else:
@@ -156,7 +151,7 @@ def tile_selfattention_pa_kernel(
             piece = w_words[(tensor, pair // (PAIRS // 2))]
             inside = 2 * PAIR * (pair % (PAIRS // 2))
             for j in range(TOKENS):
-                t = TOKENS * b + j
+                t = TOKENS * half + j
                 for g in range(PASSES):
                     nc.tensor.matmul_mx(
                         out=bank[:, j, :],
@@ -169,15 +164,15 @@ def tile_selfattention_pa_kernel(
                     )
             return bank
 
-        def in_bank_order(result):
-            return result[:].rearrange("p h j d -> p j h d")
+        def in_bank_order(result, half):
+            return result[:, :, TOKENS * half : TOKENS * (half + 1), :].rearrange("p h j d -> p j h d")
 
         def by_head(bank):
             return bank[:].rearrange("p j (h d) -> p j h d", h=2)
 
-        def add_bias(bank, result, first):
+        def add_bias(bank, result, half, first):
             nc.vector.tensor_tensor(
-                out=in_bank_order(result),
+                out=in_bank_order(result, half),
                 in0=by_head(bank),
                 in1=bias_sb[:, first : first + PAIR].rearrange("p (h d) -> p h d", h=2).unsqueeze(1).to_broadcast([P, TOKENS, 2, D]),
                 op=ALU.add,
@@ -216,36 +211,35 @@ def tile_selfattention_pa_kernel(
                     scale=shrink[:, head : head + 1], bias=shrunk_eps[:, head : head + 1],
                 )
 
-        def scale_k(bank, factor, result):
+        def scale_k(bank, factor, result, half):
             nc.vector.tensor_tensor(
-                out=in_bank_order(result),
+                out=in_bank_order(result, half),
                 in0=by_head(bank),
                 in1=factor[:, 0:SUMS].rearrange("p (j h) -> p j h", h=2).unsqueeze(3).to_broadcast([P, TOKENS, 2, D]),
                 op=ALU.mult,
             )
 
-        def scale_q(result, factor, on_vector):
+        def scale_q(result, factor, half, on_vector):
             engine = nc.vector if on_vector else nc.gpsimd
             engine.tensor_tensor(
-                out=result[:],
-                in0=result[:],
+                out=result[:, :, TOKENS * half : TOKENS * (half + 1), :],
+                in0=result[:, :, TOKENS * half : TOKENS * (half + 1), :],
                 in1=factor[:, SUMS : 2 * SUMS].rearrange("p (j h) -> p h j", h=2).unsqueeze(3).to_broadcast([P, 2, TOKENS, D]),
                 op=ALU.mult,
             )
 
-        def store(tensor, i, result):
-            b, pair = i // PAIRS, i % PAIRS
-            view = outs[tensor].rearrange("b h (p j) d -> b p h (j d)", j=TOKENS)
-            nc.sync.dma_start(out=view[b][:, 2 * pair : 2 * pair + 2, :], in_=result[:].rearrange("p h j d -> p h (j d)"))
+        def store(tensor, i):
+            pair, half = i // HALVES, i % HALVES
+            if half == HALVES - 1:
+                view = outs[tensor].rearrange("b h (p j) d -> h p b (j d)", j=TILES)
+                for h in range(2):
+                    nc.sync.dma_start(out=view[2 * pair + h], in_=res[(tensor, pair)][:, h, :, :].rearrange("p j d -> p (j d)"))
 
         def new_small(tag):
             t = small.tile([P, 2 * SUMS], F32, tag=tag, name=tag)
             return t
 
         flipped = [None] * TILES
-        lead = max(LEAD_K, LEAD_Q, LEAD_V)
-        first_step = -lead
-        last_step = UNITS - 1 - min(LEAD_K, LEAD_Q, LEAD_V) + 3
         banks, res, sm, sq = {}, {}, {}, {}
 
         def ok(i):
@@ -254,87 +248,68 @@ def tile_selfattention_pa_kernel(
         def fill(tensor, i):
             if ok(i):
                 banks[(tensor, i)] = project(tensor, i)
-                result = stage.tile([P, 2, TOKENS, D], F32, tag="result", name="result")
-                res[(tensor, i)] = result
+                if i % HALVES == 0:
+                    result = stage.tile([P, 2, TILES, D], F32, tag="result", name="result")
+                    res[(tensor, i // HALVES)] = result
 
         def fills(s):
-            fill(K, s + LEAD_K)
-            fill(Q, s + LEAD_Q)
+            fill(K, s)
+            fill(Q, s)
             fill(V, s + LEAD_V)
 
         grouped = keep.tile([P, TILES, 2 * K_PASS], BF16, align_bytes=64)
-        for t in range(TOKENS):
+        for t in range(TILES):
             flipped[t] = flip(t)
             regroup_x(flipped[t], grouped[:, t, :], t in VEC_COPY)
-            if t == 0:
-                quantise(0, 1, grouped[:, 0, :])
-            if t == 2:
-                quantise(1, 1, grouped[:, 1, :])
-                quantise(2, 1, grouped[:, 2, :])
-        quantise(3, 1, grouped[:, 3, :])
+            if t % 2 == 1:
+                quantise(t - 1, 2, grouped[:, t - 1 : t + 1, :].rearrange("p t c -> p (t c)"))
+            if t == 3:
+                spreads = [spread_bias(0), spread_bias(2)]
+                keep_bias(0, spreads[0], False)
+                keep_bias(2, spreads[1], False)
         shrink = keep.tile([P, H], F32)
         nc.vector.tensor_scalar_max(out=shrink[:], in0=raised[:], scalar1=1.0 / (MAX_SCALE * MAX_SCALE))
         shrunk_eps = keep.tile([P, H], F32)
         nc.vector.tensor_scalar(
             out=shrunk_eps[:], in0=raised[:], scalar1=1.0 / (MAX_SCALE * MAX_SCALE), scalar2=EPS_SQUARED, op0=ALU.max, op1=ALU.mult
         )
-        spreads = [spread_bias(0), spread_bias(2)]
-        keep_bias(0, spreads[0], False)
-        keep_bias(2, spreads[1], False)
+        first_step = min(0, -LEAD_V)
         fills(first_step)
+        spreads = [spread_bias(1), spread_bias(3)]
+        keep_bias(1, spreads[0], False)
+        keep_bias(3, spreads[1], False)
 
-        def part(ik, iq):
-            return (0 if ok(ik) else SUMS), (2 * SUMS if ok(iq) else SUMS)
-
-        for s in range(first_step, last_step + 1):
-            ik, iq, iv = s + LEAD_K, s + LEAD_Q, s + LEAD_V
-            u = s + lead
-            if ok(ik) or ok(iq):
-                sm[("s", s)] = new_small("sums")
-            if ok(ik - 1) or ok(iq - 1):
-                lo, hi = part(ik - 1, iq - 1)
-                sm[("e", s - 1)] = new_small("excess")
-                sm[("f", s - 1)] = new_small("factor")
-                excess_over_eps(sm[("s", s - 1)], sm[("e", s - 1)], lo, hi)
-            if ok(ik):
-                if ik % PAIRS in NARROW_K:
-                    squares_narrow(lambda j, h: banks[(K, ik)][:, j, D * h : D * (h + 1)], sm[("s", s)], 0, range(TOKENS))
+        for s in range(first_step, UNITS + 2 + max(0, -LEAD_V)):
+            i, iv = s, s + LEAD_V
+            if ok(i):
+                sm[("s", i)] = new_small("sums")
+            if ok(i - 1):
+                sm[("e", i - 1)] = new_small("excess")
+                sm[("f", i - 1)] = new_small("factor")
+                excess_over_eps(sm[("s", i - 1)], sm[("e", i - 1)], 0, 2 * SUMS)
+            if ok(i):
+                if i % 4 in NARROW_K:
+                    squares_narrow(lambda j, h: banks[(K, i)][:, j, D * h : D * (h + 1)], sm[("s", i)], 0, range(TOKENS))
                 else:
-                    sq[ik] = squares_wide(banks[(K, ik)])
-                    if FOLD and ik < NO_FOLD_FROM:
-                        fold_wide(sq[ik])
-            if ok(iq):
-                add_bias(banks[(Q, iq)], res[(Q, iq)], PAIR * (iq % PAIRS))
-            if ok(ik) and ik >= NO_FOLD_FROM and ik % PAIRS not in NARROW_K:
-                reduce_wide(sq[ik], sm[("s", s)], D)
+                    sq[i] = squares_wide(banks[(K, i)])
+                    if FOLD and i < NO_FOLD_FROM:
+                        fold_wide(sq[i])
+                add_bias(banks[(Q, i)], res[(Q, i // HALVES)], i % HALVES, PAIR * (i // HALVES))
+            if ok(i) and i >= NO_FOLD_FROM and i % 4 not in NARROW_K:
+                reduce_wide(sq[i], sm[("s", i)], D)
             if ok(iv):
-                add_bias(banks[(V, iv)], res[(V, iv)], C + PAIR * (iv % PAIRS))
-                store(V, iv, res[(V, iv)])
+                add_bias(banks[(V, iv)], res[(V, iv // HALVES)], iv % HALVES, C + PAIR * (iv // HALVES))
+                store(V, iv)
             fills(s + 1)
-            if u in FLIP_AT:
-                flipped[FLIP_AT[u]] = flip(FLIP_AT[u])
-            extra = None
-            if u == 1:
-                extra = spread_bias(1)
-            if u == 2:
-                extra = spread_bias(3)
-            if u == QUANT_AT:
-                quantise(TOKENS, TOKENS, grouped[:, TOKENS:TILES, :].rearrange("p t c -> p (t c)"))
-            if ok(ik - 1):
-                k_factors(sm[("e", s - 1)], sm[("f", s - 1)])
-                scale_k(banks[(K, ik - 1)], sm[("f", s - 1)], res[(K, ik - 1)])
-                store(K, ik - 1, res[(K, ik - 1)])
-            if ok(iq - 1):
-                q_factors(sm[("e", s - 1)], sm[("f", s - 1)], (iq - 1) % PAIRS)
-                scale_q(res[(Q, iq - 1)], sm[("f", s - 1)], iq - 1 >= VECTOR_Q_FROM)
-                store(Q, iq - 1, res[(Q, iq - 1)])
-            if ok(iq):
-                squares_narrow(lambda j, h: res[(Q, iq)][:, h, j, :], sm[("s", s)], SUMS, range(TOKENS))
-            if u in FLIP_AT:
-                regroup_x(flipped[FLIP_AT[u]], grouped[:, FLIP_AT[u], :], False)
-            if u == 1:
-                keep_bias(1, extra, False)
-            if u == 2:
-                keep_bias(3, extra, False)
-            if ok(ik) and ik < NO_FOLD_FROM and ik % PAIRS not in NARROW_K:
-                reduce_wide(sq[ik], sm[("s", s)], D // 2 if FOLD else D)
+            if ok(i - 1):
+                k_factors(sm[("e", i - 1)], sm[("f", i - 1)])
+                scale_k(banks[(K, i - 1)], sm[("f", i - 1)], res[(K, (i - 1) // HALVES)], (i - 1) % HALVES)
+                store(K, i - 1)
+                q_factors(sm[("e", i - 1)], sm[("f", i - 1)], (i - 1) // HALVES)
+                scale_q(res[(Q, (i - 1) // HALVES)], sm[("f", i - 1)], (i - 1) % HALVES, i - 1 >= VECTOR_Q_FROM)
+                store(Q, i - 1)
+            if ok(i):
+                half = i % HALVES
+                squares_narrow(lambda j, h: res[(Q, i // HALVES)][:, h, TOKENS * half + j, :], sm[("s", i)], SUMS, range(TOKENS))
+            if ok(i) and i < NO_FOLD_FROM and i % 4 not in NARROW_K:
+                reduce_wide(sq[i], sm[("s", i)], D // 2 if FOLD else D)

@@ -28,7 +28,7 @@ Q, K, V = 0, 1, 2
 MAX_SCALE = 100.0
 EPS_SQUARED = 1.0e-24
 
-NARROW_K = ()
+NARROW_K = (0, 2)
 FOLD = True
 LEAD_V = 1
 VECTOR_Q_FROM = 16

@@ -31,6 +31,8 @@ EPS_SQUARED = 1.0e-24
 NARROW_K = (0, 2)
 FOLD = True
 LEAD_V = 1
+WARM_UPS = 5
+SPREAD_AFTER = {1: 2, 3: 0, 5: 3, 7: 1}
 VECTOR_Q_FROM = 16
 NO_FOLD_FROM = 15
 LATER_BIAS = {}
@@ -52,12 +54,17 @@ def tile_selfattention_pa_kernel(
         warm = keep.tile([P, 4], F32)
         nc.vector.memset(warm[:], 1.0)
         nc.scalar.activation(out=warm[:, 1:2], in_=warm[:, 0:1], func=ACT.Exp)
+        ones = keep.tile([P, P], BF16)
+        nc.vector.memset(ones[:], 1.0)
+        idle_rhs = keep.tile([P, BANK], BF16)
+        nc.vector.memset(idle_rhs[:], 1.0)
         rows = keep.tile([P, 2 * C], BF16)
         nc.vector.memset(rows[:].bitcast(I32), 0)
         w_planes = keep.tile([P, PASSES, 3 * C], U8, align_bytes=64)
         nc.vector.memset(w_planes[:].rearrange("p g n -> p (g n)").bitcast(I32), 0)
-        ones = keep.tile([P, P], BF16)
-        nc.vector.memset(ones[:], 1.0)
+        idle_bank = psum.tile([P, BANK], F32, tag="brief", name="idle_bank")
+        for n in range(WARM_UPS):
+            nc.tensor.matmul(idle_bank[:], lhsT=ones[:], rhs=idle_rhs[:], start=True, stop=True)
         ident = keep.tile([P, P], F32)
         make_identity(nc, ident[:])
 
@@ -263,10 +270,11 @@ def tile_selfattention_pa_kernel(
             regroup_x(flipped[t], grouped[:, t, :], t in VEC_COPY)
             if t % 2 == 1:
                 quantise(t - 1, 2, grouped[:, t - 1 : t + 1, :].rearrange("p t c -> p (t c)"))
-            if t == 3:
-                spreads = [spread_bias(0), spread_bias(2)]
-                keep_bias(0, spreads[0], False)
-                keep_bias(2, spreads[1], False)
+            if t == 1:
+                nc.vector.tensor_copy(out=warm[:, 3:4], in_=idle_bank[:, 0:1])
+            if t in SPREAD_AFTER:
+                piece = SPREAD_AFTER[t]
+                keep_bias(piece, spread_bias(piece), False)
         shrink = keep.tile([P, H], F32)
         nc.vector.tensor_scalar_max(out=shrink[:], in0=raised[:], scalar1=1.0 / (MAX_SCALE * MAX_SCALE))
         shrunk_eps = keep.tile([P, H], F32)
@@ -275,9 +283,6 @@ def tile_selfattention_pa_kernel(
         )
         first_step = min(0, -LEAD_V)
         fills(first_step)
-        spreads = [spread_bias(1), spread_bias(3)]
-        keep_bias(1, spreads[0], False)
-        keep_bias(3, spreads[1], False)
 
         for s in range(first_step, UNITS + 2 + max(0, -LEAD_V)):
             i, iv = s, s + LEAD_V

@@ -62,7 +62,7 @@ def tile_selfattention_pa_kernel(
         nc.vector.memset(rows[:].bitcast(I32), 0)
         w_planes = keep.tile([P, PASSES, 3 * C], U8, align_bytes=64)
         nc.vector.memset(w_planes[:].rearrange("p g n -> p (g n)").bitcast(I32), 0)
-        idle_bank = psum.tile([P, BANK], F32, tag="brief", name="idle_bank")
+        idle_bank = psum_k.tile([P, BANK], F32, tag="held", name="idle_bank")
         for n in range(WARM_UPS):
             nc.tensor.matmul(idle_bank[:], lhsT=ones[:], rhs=idle_rhs[:], start=True, stop=True)
         ident = keep.tile([P, P], F32)
@@ -270,7 +270,9 @@ def tile_selfattention_pa_kernel(
             regroup_x(flipped[t], grouped[:, t, :], t in VEC_COPY)
             if t % 2 == 1:
                 quantise(t - 1, 2, grouped[:, t - 1 : t + 1, :].rearrange("p t c -> p (t c)"))
-            if t == 1:
+            if t % 2 == 0:
+                nc.tensor.matmul(idle_bank[:], lhsT=ones[:], rhs=idle_rhs[:], start=True, stop=True)
+            if t == TILES - 2:
                 nc.vector.tensor_copy(out=warm[:, 3:4], in_=idle_bank[:, 0:1])
             if t in SPREAD_AFTER:
                 piece = SPREAD_AFTER[t]

@@ -50,7 +50,7 @@ def tile_selfattention_pa_kernel(
         name="stage", bufs=12
     ) as stage, tc.tile_pool(name="scratch", bufs=3) as scratch, tc.tile_pool(name="small", bufs=4) as small, tc.psum_pool(
         name="psum", bufs=5
-    ) as psum, tc.psum_pool(name="psum_k", bufs=3) as psum_k:
+    ) as psum, tc.psum_pool(name="psum_k", bufs=3) as psum_k, tc.manual_schedule():
         warm = keep.tile([P, 4], F32)
         nc.vector.memset(warm[:], 1.0)
         nc.scalar.activation(out=warm[:, 1:2], in_=warm[:, 0:1], func=ACT.Exp)
@@ -87,23 +87,22 @@ def tile_selfattention_pa_kernel(
             w_words[(tensor, half)] = piece
 
         logs = keep.tile([P, H], BF16)
-        with tc.manual_schedule(engines={mybir.EngineType.SP}):
-            nc.sync.dma_start(out=logs[:], in_=log_scale_mul.rearrange("a h b c -> (a h b c)").partition_broadcast(P))
-            load_x(0, 1)
-            load_x(1, 1)
-            nc.sync.dma_start(out=rows[0:1, 0:C], in_=q_bias.rearrange("(o n) -> o n", o=1))
-            nc.sync.dma_start(out=rows[0:1, C : 2 * C], in_=v_bias.rearrange("(o n) -> o n", o=1))
-            load_x(2, 2)
-            load_x(4, 2)
-            load_x(6, 2)
-            for r in range(4):
-                nc.sync.dma_start(
-                    out=w_planes[r:P:32, :, :].bitcast(I32),
-                    in_=W_qkv_scales[:, r:16:4, :].rearrange("g q n -> q g n").bitcast(I32),
-                )
-            for half in range(2):
-                for tensor in (V, K, Q):
-                    load_w(tensor, half)
+        nc.sync.dma_start(out=logs[:], in_=log_scale_mul.rearrange("a h b c -> (a h b c)").partition_broadcast(P))
+        load_x(0, 1)
+        load_x(1, 1)
+        nc.sync.dma_start(out=rows[0:1, 0:C], in_=q_bias.rearrange("(o n) -> o n", o=1))
+        nc.sync.dma_start(out=rows[0:1, C : 2 * C], in_=v_bias.rearrange("(o n) -> o n", o=1))
+        load_x(2, 2)
+        load_x(4, 2)
+        load_x(6, 2)
+        for r in range(4):
+            nc.sync.dma_start(
+                out=w_planes[r:P:32, :, :].bitcast(I32),
+                in_=W_qkv_scales[:, r:16:4, :].rearrange("g q n -> q g n").bitcast(I32),
+            )
+        for half in range(2):
+            for tensor in (V, K, Q):
+                load_w(tensor, half)
         raised = keep.tile([P, H], F32)
         nc.scalar.activation(out=raised[:], in_=logs[:], func=ACT.Exp, scale=-2.0)
         nc.scalar.activation(out=warm[:, 2:3], in_=raised[:, 0:1], func=ACT.Abs_reciprocal_sqrt)
@@ -293,15 +292,24 @@ def tile_selfattention_pa_kernel(
             if ok(i - 1):
                 sm[("e", i - 1)] = new_small("excess")
                 sm[("f", i - 1)] = new_small("factor")
-                excess_over_eps(sm[("s", i - 1)], sm[("e", i - 1)], 0, 2 * SUMS)
             if ok(i):
+                add_bias(banks[(Q, i)], res[(Q, i // HALVES)], i % HALVES, PAIR * (i // HALVES))
                 if i % 4 in NARROW_K:
-                    squares_narrow(lambda j, h: banks[(K, i)][:, j, D * h : D * (h + 1)], sm[("s", i)], 0, range(TOKENS))
+                    squares_narrow(lambda j, h: banks[(K, i)][:, j, D * h : D * (h + 1)], sm[("s", i)], 0, range(2))
                 else:
                     sq[i] = squares_wide(banks[(K, i)])
                     if FOLD and i < NO_FOLD_FROM:
                         fold_wide(sq[i])
-                add_bias(banks[(Q, i)], res[(Q, i // HALVES)], i % HALVES, PAIR * (i // HALVES))
+            if ok(i - 1):
+                excess_over_eps(sm[("s", i - 1)], sm[("e", i - 1)], 0, 2 * SUMS)
+            if ok(i):
+                half = i % HALVES
+                if i % 4 in NARROW_K:
+                    squares_narrow(lambda j, h: banks[(K, i)][:, j, D * h : D * (h + 1)], sm[("s", i)], 0, range(2, TOKENS))
+                    qa = 0
+                else:
+                    qa = 1
+                squares_narrow(lambda j, h: res[(Q, i // HALVES)][:, h, TOKENS * half + j, :], sm[("s", i)], SUMS, range(qa))
             if ok(i) and i >= NO_FOLD_FROM and i % 4 not in NARROW_K:
                 reduce_wide(sq[i], sm[("s", i)], D)
             if ok(iv):
@@ -316,7 +324,6 @@ def tile_selfattention_pa_kernel(
                 scale_q(res[(Q, (i - 1) // HALVES)], sm[("f", i - 1)], (i - 1) % HALVES, i - 1 >= VECTOR_Q_FROM)
                 store(Q, i - 1)
             if ok(i):
-                half = i % HALVES
-                squares_narrow(lambda j, h: res[(Q, i // HALVES)][:, h, TOKENS * half + j, :], sm[("s", i)], SUMS, range(TOKENS))
+                squares_narrow(lambda j, h: res[(Q, i // HALVES)][:, h, TOKENS * half + j, :], sm[("s", i)], SUMS, range(qa, TOKENS))
             if ok(i) and i < NO_FOLD_FROM and i % 4 not in NARROW_K:
                 reduce_wide(sq[i], sm[("s", i)], D // 2 if FOLD else D)

@@ -30,12 +30,13 @@ EPS_SQUARED = 1.0e-24
 
 NARROW_K = (0, 2)
 FOLD = True
-LEAD_V = 1
-WARM_UPS = 5
-SPREAD_AFTER = {1: 2, 3: 0, 5: 3, 7: 1}
+LEAD_V = -1
+WARM_UPS = 4
+CREDITS = {1: 2, 3: 0, 5: 3, 7: 1}
+BIAS_AFTER = {1: 2, 3: 0, 5: 3, 7: 1}
+QUANTISE_AFTER = {2: (0, 2), 4: (2, 2), 5: (4, 1), 6: (5, 1), 7: (6, 1)}
 VECTOR_Q_FROM = 16
 NO_FOLD_FROM = 15
-LATER_BIAS = {}
 VEC_COPY = (0, 2, 4, 6)
 
 FLOPS = 2 * B * L * C * 3 * C
@@ -48,7 +49,7 @@ def tile_selfattention_pa_kernel(
     outs = (out_0, out_1, out_2)
     with tc.tile_pool(name="keep", bufs=1) as keep, tc.tile_pool(name="regroup", bufs=4) as regroup, tc.tile_pool(
         name="stage", bufs=12
-    ) as stage, tc.tile_pool(name="scratch", bufs=3) as scratch, tc.tile_pool(name="small", bufs=4) as small, tc.psum_pool(
+    ) as stage, tc.tile_pool(name="scratch", bufs=3) as scratch, tc.tile_pool(name="small", bufs=4) as small, tc.tile_pool(name="junk", bufs=16) as junk, tc.psum_pool(
         name="psum", bufs=5
     ) as psum, tc.psum_pool(name="psum_k", bufs=3) as psum_k, tc.manual_schedule():
         warm = keep.tile([P, 4], F32)
@@ -57,11 +58,13 @@ def tile_selfattention_pa_kernel(
         ones = keep.tile([P, P], BF16)
         nc.vector.memset(ones[:], 1.0)
         idle_rhs = keep.tile([P, BANK], BF16)
-        nc.vector.memset(idle_rhs[:], 1.0)
+        nc.gpsimd.memset(idle_rhs[:], 1.0)
         rows = keep.tile([P, 2 * C], BF16)
         nc.vector.memset(rows[:].bitcast(I32), 0)
-        w_planes = keep.tile([P, PASSES, 3 * C], U8, align_bytes=64)
-        nc.vector.memset(w_planes[:].rearrange("p g n -> p (g n)").bitcast(I32), 0)
+        qk_planes = keep.tile([P, PASSES, 2 * C], U8, align_bytes=64)
+        nc.vector.memset(qk_planes[:].rearrange("p g n -> p (g n)").bitcast(I32), 0)
+        v_planes = keep.tile([P, PASSES, C], U8, align_bytes=64)
+        nc.vector.memset(v_planes[:].rearrange("p g n -> p (g n)").bitcast(I32), 0)
         idle_bank = psum_k.tile([P, BANK], F32, tag="held", name="idle_bank")
         for n in range(WARM_UPS):
             nc.tensor.matmul(idle_bank[:], lhsT=ones[:], rhs=idle_rhs[:], start=True, stop=True)
@@ -86,6 +89,13 @@ def tile_selfattention_pa_kernel(
             nc.sync.dma_start(out=piece[:].bitcast(I32), in_=w_view[:, :, first : first + C].bitcast(I32))
             w_words[(tensor, half)] = piece
 
+        def load_planes(planes, first, count):
+            for r in range(4):
+                nc.sync.dma_start(
+                    out=planes[r:P:32, :, :].bitcast(I32),
+                    in_=W_qkv_scales[:, r:16:4, first : first + count].rearrange("g q n -> q g n").bitcast(I32),
+                )
+
         logs = keep.tile([P, H], BF16)
         nc.sync.dma_start(out=logs[:], in_=log_scale_mul.rearrange("a h b c -> (a h b c)").partition_broadcast(P))
         load_x(0, 1)
@@ -94,17 +104,18 @@ def tile_selfattention_pa_kernel(
         nc.sync.dma_start(out=rows[0:1, C : 2 * C], in_=v_bias.rearrange("(o n) -> o n", o=1))
         load_x(2, 2)
         load_x(4, 2)
-        load_x(6, 2)
-        for r in range(4):
-            nc.sync.dma_start(
-                out=w_planes[r:P:32, :, :].bitcast(I32),
-                in_=W_qkv_scales[:, r:16:4, :].rearrange("g q n -> q g n").bitcast(I32),
-            )
-        for half in range(2):
-            for tensor in (V, K, Q):
-                load_w(tensor, half)
+        load_x(6, 1)
+        load_x(7, 1)
+        load_planes(qk_planes, 0, 2 * C)
+        load_w(K, 0)
+        load_w(Q, 0)
+        load_planes(v_planes, 2 * C, C)
+        load_w(V, 0)
+        load_w(K, 1)
+        load_w(Q, 1)
+        load_w(V, 1)
         raised = keep.tile([P, H], F32)
-        nc.scalar.activation(out=raised[:], in_=logs[:], func=ACT.Exp, scale=-2.0)
+        nc.scalar.activation(out=raised[:], in_=logs[:], func=ACT.Exp)
         nc.scalar.activation(out=warm[:, 2:3], in_=raised[:, 0:1], func=ACT.Abs_reciprocal_sqrt)
 
         x_words = x_sb[:].bitcast(F32)
@@ -133,10 +144,10 @@ def tile_selfattention_pa_kernel(
                 in_=grouped,
             )
 
-        bias_sb = keep.tile([P, 2 * C], F32)
+        bias_sb = keep.tile([P, 2 * C], BF16)
 
         def spread_bias(piece):
-            spread = psum.tile([P, BANK], F32, tag="brief", name="spread")
+            spread = psum_k.tile([P, BANK], BF16, tag="held", name="spread")
             nc.tensor.matmul(spread[:], lhsT=ones[:], rhs=rows[:, BANK * piece : BANK * (piece + 1)], start=True, stop=True)
             return spread
 
@@ -153,7 +164,7 @@ def tile_selfattention_pa_kernel(
                 bank = psum_k.tile([P, TOKENS, PAIR], F32, tag="held", name="bank")
             else:
                 bank = psum.tile([P, TOKENS, PAIR], F32, tag="brief", name="bank")
-            col = C * tensor + PAIR * pair
+            planes, col = (v_planes, PAIR * pair) if tensor == V else (qk_planes, C * tensor + PAIR * pair)
             piece = w_words[(tensor, pair // (PAIRS // 2))]
             inside = 2 * PAIR * (pair % (PAIRS // 2))
             for j in range(TOKENS):
@@ -164,7 +175,7 @@ def tile_selfattention_pa_kernel(
                         lhsT=x_codes[:, t, g, :].bitcast(FP8X4),
                         lhsT_scale=x_planes[:, t, g, :],
                         rhs=piece[:, g, inside : inside + 2 * PAIR].bitcast(FP4X4),
-                        rhs_scale=w_planes[:, g, col : col + PAIR],
+                        rhs_scale=planes[:, g, col : col + PAIR],
                         start=(g == 0),
                         stop=(g == PASSES - 1),
                     )
@@ -187,7 +198,7 @@ def tile_selfattention_pa_kernel(
         def squares_narrow(vector_of, sums, first, tokens):
             for j in tokens:
                 for h in range(2):
-                    unused = small.tile([P, D], BF16, tag="unused", name="unused")
+                    unused = junk.tile([P, D], BF16, tag="unused", name="unused")
                     nc.scalar.activation(out=unused[:], in_=vector_of(j, h), func=ACT.Square, accum_out=sums[:, first + 2 * j + h : first + 2 * j + h + 1])
 
         def squares_wide(bank):
@@ -206,16 +217,16 @@ def tile_selfattention_pa_kernel(
         def excess_over_eps(sums, excess, lo, hi):
             nc.scalar.activation(out=excess[:, lo:hi], in_=sums[:, lo:hi], func=ACT.Relu, bias=-EPS_SQUARED)
 
-        def k_factors(excess, factor):
-            nc.scalar.activation(out=factor[:, 0:SUMS], in_=excess[:, 0:SUMS], func=ACT.Abs_reciprocal_sqrt, bias=EPS_SQUARED)
+        def inverse_norms(excess, factor):
+            nc.scalar.activation(out=factor[:], in_=excess[:], func=ACT.Abs_reciprocal_sqrt, bias=EPS_SQUARED)
 
-        def q_factors(excess, factor, pair):
-            for h in range(2):
-                head = 2 * pair + h
-                nc.scalar.activation(
-                    out=factor[:, SUMS + h : 2 * SUMS : 2], in_=excess[:, SUMS + h : 2 * SUMS : 2], func=ACT.Abs_reciprocal_sqrt,
-                    scale=shrink[:, head : head + 1], bias=shrunk_eps[:, head : head + 1],
-                )
+        def q_multipliers(factor, pair):
+            nc.gpsimd.tensor_tensor(
+                out=factor[:, SUMS : 2 * SUMS].rearrange("p (j h) -> p j h", h=2),
+                in0=factor[:, SUMS : 2 * SUMS].rearrange("p (j h) -> p j h", h=2),
+                in1=multiplier[:, 2 * pair : 2 * pair + 2].unsqueeze(1).to_broadcast([P, TOKENS, 2]),
+                op=ALU.mult,
+            )
 
         def scale_k(bank, factor, result, half):
             nc.vector.tensor_tensor(
@@ -264,28 +275,39 @@ def tile_selfattention_pa_kernel(
             fill(V, s + LEAD_V)
 
         grouped = keep.tile([P, TILES, 2 * K_PASS], BF16, align_bytes=64)
+        spreads = {}
+
+        def credit(piece):
+            if piece is None:
+                nc.tensor.matmul(idle_bank[:], lhsT=ones[:], rhs=idle_rhs[:], start=True, stop=True)
+            else:
+                spreads[piece] = spread_bias(piece)
+
+        def keep_piece(piece):
+            keep_bias(piece, spreads[piece], False)
+
+        def quantise_some(t, count):
+            quantise(t, count, grouped[:, t : t + count, :].rearrange("p t c -> p (t c)"))
+
+        nc.vector.tensor_copy(out=warm[:, 3:4], in_=idle_bank[:, 0:1])
         for t in range(TILES):
             flipped[t] = flip(t)
+            if t in CREDITS:
+                credit(CREDITS[t])
             regroup_x(flipped[t], grouped[:, t, :], t in VEC_COPY)
-            if t % 2 == 1:
-                quantise(t - 1, 2, grouped[:, t - 1 : t + 1, :].rearrange("p t c -> p (t c)"))
-            if t % 2 == 0:
-                nc.tensor.matmul(idle_bank[:], lhsT=ones[:], rhs=idle_rhs[:], start=True, stop=True)
-            if t == TILES - 2:
-                nc.vector.tensor_copy(out=warm[:, 3:4], in_=idle_bank[:, 0:1])
-            if t in SPREAD_AFTER:
-                piece = SPREAD_AFTER[t]
-                keep_bias(piece, spread_bias(piece), False)
-        shrink = keep.tile([P, H], F32)
-        nc.vector.tensor_scalar_max(out=shrink[:], in0=raised[:], scalar1=1.0 / (MAX_SCALE * MAX_SCALE))
-        shrunk_eps = keep.tile([P, H], F32)
-        nc.vector.tensor_scalar(
-            out=shrunk_eps[:], in0=raised[:], scalar1=1.0 / (MAX_SCALE * MAX_SCALE), scalar2=EPS_SQUARED, op0=ALU.max, op1=ALU.mult
-        )
-        first_step = min(0, -LEAD_V)
-        fills(first_step)
+            if t in BIAS_AFTER:
+                keep_piece(BIAS_AFTER[t])
+            if t in QUANTISE_AFTER:
+                quantise_some(*QUANTISE_AFTER[t])
+        quantise_some(7, 1)
+        multiplier = keep.tile([P, H], F32)
+        nc.vector.tensor_scalar_min(out=multiplier[:], in0=raised[:], scalar1=MAX_SCALE)
+        fill(K, 0)
+        fill(Q, 0)
+        for v in range(0):
+            fill(V, v)
 
-        for s in range(first_step, UNITS + 2 + max(0, -LEAD_V)):
+        for s in range(UNITS + 2):
             i, iv = s, s + LEAD_V
             if ok(i):
                 sm[("s", i)] = new_small("sums")
@@ -317,10 +339,10 @@ def tile_selfattention_pa_kernel(
                 store(V, iv)
             fills(s + 1)
             if ok(i - 1):
-                k_factors(sm[("e", i - 1)], sm[("f", i - 1)])
+                inverse_norms(sm[("e", i - 1)], sm[("f", i - 1)])
                 scale_k(banks[(K, i - 1)], sm[("f", i - 1)], res[(K, (i - 1) // HALVES)], (i - 1) % HALVES)
                 store(K, i - 1)
-                q_factors(sm[("e", i - 1)], sm[("f", i - 1)], (i - 1) // HALVES)
+                q_multipliers(sm[("f", i - 1)], (i - 1) // HALVES)
                 scale_q(res[(Q, (i - 1) // HALVES)], sm[("f", i - 1)], (i - 1) % HALVES, i - 1 >= VECTOR_Q_FROM)
                 store(Q, i - 1)
             if ok(i):

@@ -30,9 +30,10 @@ EPS_SQUARED = 1.0e-24
 
 NARROW_K = (0, 2)
 FOLD = True
-LEAD_V = -1
-WARM_UPS = 4
-CREDITS = {1: 2, 3: 0, 5: 3, 7: 1}
+LEAD_V = 0
+IDLE = 384
+WARM_UPS = 5
+CREDITS = {0: None, 1: 2, 2: None, 3: 0, 4: None, 5: 3, 6: None, 7: 1}
 BIAS_AFTER = {1: 2, 3: 0, 5: 3, 7: 1}
 QUANTISE_AFTER = {2: (0, 2), 4: (2, 2), 5: (4, 1), 6: (5, 1), 7: (6, 1)}
 VECTOR_Q_FROM = 16
@@ -61,10 +62,8 @@ def tile_selfattention_pa_kernel(
         nc.gpsimd.memset(idle_rhs[:], 1.0)
         rows = keep.tile([P, 2 * C], BF16)
         nc.vector.memset(rows[:].bitcast(I32), 0)
-        qk_planes = keep.tile([P, PASSES, 2 * C], U8, align_bytes=64)
-        nc.vector.memset(qk_planes[:].rearrange("p g n -> p (g n)").bitcast(I32), 0)
-        v_planes = keep.tile([P, PASSES, C], U8, align_bytes=64)
-        nc.vector.memset(v_planes[:].rearrange("p g n -> p (g n)").bitcast(I32), 0)
+        w_planes = keep.tile([P, PASSES, 3 * C], U8, align_bytes=64)
+        nc.vector.memset(w_planes[:].rearrange("p g n -> p (g n)").bitcast(I32), 0)
         idle_bank = psum_k.tile([P, BANK], F32, tag="held", name="idle_bank")
         for n in range(WARM_UPS):
             nc.tensor.matmul(idle_bank[:], lhsT=ones[:], rhs=idle_rhs[:], start=True, stop=True)
@@ -89,13 +88,6 @@ def tile_selfattention_pa_kernel(
             nc.sync.dma_start(out=piece[:].bitcast(I32), in_=w_view[:, :, first : first + C].bitcast(I32))
             w_words[(tensor, half)] = piece
 
-        def load_planes(planes, first, count):
-            for r in range(4):
-                nc.sync.dma_start(
-                    out=planes[r:P:32, :, :].bitcast(I32),
-                    in_=W_qkv_scales[:, r:16:4, first : first + count].rearrange("g q n -> q g n").bitcast(I32),
-                )
-
         logs = keep.tile([P, H], BF16)
         nc.sync.dma_start(out=logs[:], in_=log_scale_mul.rearrange("a h b c -> (a h b c)").partition_broadcast(P))
         load_x(0, 1)
@@ -106,10 +98,13 @@ def tile_selfattention_pa_kernel(
         load_x(4, 2)
         load_x(6, 1)
         load_x(7, 1)
-        load_planes(qk_planes, 0, 2 * C)
+        for r in range(4):
+            nc.sync.dma_start(
+                out=w_planes[r:P:32, :, :].bitcast(I32),
+                in_=W_qkv_scales[:, r:16:4, :].rearrange("g q n -> q g n").bitcast(I32),
+            )
         load_w(K, 0)
         load_w(Q, 0)
-        load_planes(v_planes, 2 * C, C)
         load_w(V, 0)
         load_w(K, 1)
         load_w(Q, 1)
@@ -147,7 +142,7 @@ def tile_selfattention_pa_kernel(
         bias_sb = keep.tile([P, 2 * C], BF16)
 
         def spread_bias(piece):
-            spread = psum_k.tile([P, BANK], BF16, tag="held", name="spread")
+            spread = psum.tile([P, BANK], BF16, tag="brief", name="spread")
             nc.tensor.matmul(spread[:], lhsT=ones[:], rhs=rows[:, BANK * piece : BANK * (piece + 1)], start=True, stop=True)
             return spread
 
@@ -164,7 +159,7 @@ def tile_selfattention_pa_kernel(
                 bank = psum_k.tile([P, TOKENS, PAIR], F32, tag="held", name="bank")
             else:
                 bank = psum.tile([P, TOKENS, PAIR], F32, tag="brief", name="bank")
-            planes, col = (v_planes, PAIR * pair) if tensor == V else (qk_planes, C * tensor + PAIR * pair)
+            col = C * tensor + PAIR * pair
             piece = w_words[(tensor, pair // (PAIRS // 2))]
             inside = 2 * PAIR * (pair % (PAIRS // 2))
             for j in range(TOKENS):
@@ -175,7 +170,7 @@ def tile_selfattention_pa_kernel(
                         lhsT=x_codes[:, t, g, :].bitcast(FP8X4),
                         lhsT_scale=x_planes[:, t, g, :],
                         rhs=piece[:, g, inside : inside + 2 * PAIR].bitcast(FP4X4),
-                        rhs_scale=planes[:, g, col : col + PAIR],
+                        rhs_scale=w_planes[:, g, col : col + PAIR],
                         start=(g == 0),
                         stop=(g == PASSES - 1),
                     )
@@ -279,7 +274,7 @@ def tile_selfattention_pa_kernel(
 
         def credit(piece):
             if piece is None:
-                nc.tensor.matmul(idle_bank[:], lhsT=ones[:], rhs=idle_rhs[:], start=True, stop=True)
+                nc.tensor.matmul(idle_bank[:, 0:IDLE], lhsT=ones[:], rhs=idle_rhs[:, 0:IDLE], start=True, stop=True)
             else:
                 spreads[piece] = spread_bias(piece)
 
@@ -289,7 +284,6 @@ def tile_selfattention_pa_kernel(
         def quantise_some(t, count):
             quantise(t, count, grouped[:, t : t + count, :].rearrange("p t c -> p (t c)"))
 
-        nc.vector.tensor_copy(out=warm[:, 3:4], in_=idle_bank[:, 0:1])
         for t in range(TILES):
             flipped[t] = flip(t)
             if t in CREDITS:
@@ -299,12 +293,15 @@ def tile_selfattention_pa_kernel(
                 keep_piece(BIAS_AFTER[t])
             if t in QUANTISE_AFTER:
                 quantise_some(*QUANTISE_AFTER[t])
+        for n in range(2):
+            credit(None)
         quantise_some(7, 1)
+        nc.vector.tensor_copy(out=warm[:, 3:4], in_=idle_bank[:, 0:1])
         multiplier = keep.tile([P, H], F32)
         nc.vector.tensor_scalar_min(out=multiplier[:], in0=raised[:], scalar1=MAX_SCALE)
         fill(K, 0)
         fill(Q, 0)
-        for v in range(0):
+        for v in range(1):
             fill(V, v)
 
         for s in range(UNITS + 2):

@@ -30,13 +30,12 @@ EPS_SQUARED = 1.0e-24
 
 NARROW_K = (0, 2)
 FOLD = True
-LEAD_V = 0
 IDLE = 384
 WARM_UPS = 5
-CREDITS = {0: None, 1: 2, 2: None, 3: 0, 4: None, 5: 3, 6: None, 7: 1}
+CREDITS = {0: 2, 1: None, 2: 0, 3: None, 4: 3, 5: None, 6: 1}
 BIAS_AFTER = {1: 2, 3: 0, 5: 3, 7: 1}
 QUANTISE_AFTER = {2: (0, 2), 4: (2, 2), 5: (4, 1), 6: (5, 1), 7: (6, 1)}
-VECTOR_Q_FROM = 16
+VECTOR_Q_FROM = 15
 NO_FOLD_FROM = 15
 VEC_COPY = (0, 2, 4, 6)
 
@@ -50,7 +49,7 @@ def tile_selfattention_pa_kernel(
     outs = (out_0, out_1, out_2)
     with tc.tile_pool(name="keep", bufs=1) as keep, tc.tile_pool(name="regroup", bufs=4) as regroup, tc.tile_pool(
         name="stage", bufs=12
-    ) as stage, tc.tile_pool(name="scratch", bufs=3) as scratch, tc.tile_pool(name="small", bufs=4) as small, tc.tile_pool(name="junk", bufs=16) as junk, tc.psum_pool(
+    ) as stage, tc.tile_pool(name="scratch", bufs=3) as scratch, tc.tile_pool(name="small", bufs=4) as small, tc.psum_pool(
         name="psum", bufs=5
     ) as psum, tc.psum_pool(name="psum_k", bufs=3) as psum_k, tc.manual_schedule():
         warm = keep.tile([P, 4], F32)
@@ -62,8 +61,10 @@ def tile_selfattention_pa_kernel(
         nc.gpsimd.memset(idle_rhs[:], 1.0)
         rows = keep.tile([P, 2 * C], BF16)
         nc.vector.memset(rows[:].bitcast(I32), 0)
-        w_planes = keep.tile([P, PASSES, 3 * C], U8, align_bytes=64)
-        nc.vector.memset(w_planes[:].rearrange("p g n -> p (g n)").bitcast(I32), 0)
+        qk_planes = keep.tile([P, PASSES, 2 * C], U8, align_bytes=64)
+        nc.vector.memset(qk_planes[:].rearrange("p g n -> p (g n)").bitcast(I32), 0)
+        v_planes = keep.tile([P, PASSES, C], U8, align_bytes=64)
+        nc.vector.memset(v_planes[:].rearrange("p g n -> p (g n)").bitcast(I32), 0)
         idle_bank = psum_k.tile([P, BANK], F32, tag="held", name="idle_bank")
         for n in range(WARM_UPS):
             nc.tensor.matmul(idle_bank[:], lhsT=ones[:], rhs=idle_rhs[:], start=True, stop=True)
@@ -88,6 +89,13 @@ def tile_selfattention_pa_kernel(
             nc.sync.dma_start(out=piece[:].bitcast(I32), in_=w_view[:, :, first : first + C].bitcast(I32))
             w_words[(tensor, half)] = piece
 
+        def load_planes(planes, first, count):
+            for r in range(4):
+                nc.sync.dma_start(
+                    out=planes[r:P:32, :, :].bitcast(I32),
+                    in_=W_qkv_scales[:, r:16:4, first : first + count].rearrange("g q n -> q g n").bitcast(I32),
+                )
+
         logs = keep.tile([P, H], BF16)
         nc.sync.dma_start(out=logs[:], in_=log_scale_mul.rearrange("a h b c -> (a h b c)").partition_broadcast(P))
         load_x(0, 1)
@@ -98,20 +106,23 @@ def tile_selfattention_pa_kernel(
         load_x(4, 2)
         load_x(6, 1)
         load_x(7, 1)
-        for r in range(4):
-            nc.sync.dma_start(
-                out=w_planes[r:P:32, :, :].bitcast(I32),
-                in_=W_qkv_scales[:, r:16:4, :].rearrange("g q n -> q g n").bitcast(I32),
-            )
+        load_planes(qk_planes, 0, 2 * C)
         load_w(K, 0)
         load_w(Q, 0)
+        load_planes(v_planes, 2 * C, C)
         load_w(V, 0)
         load_w(K, 1)
         load_w(Q, 1)
         load_w(V, 1)
         raised = keep.tile([P, H], F32)
-        nc.scalar.activation(out=raised[:], in_=logs[:], func=ACT.Exp)
+        nc.scalar.activation(out=raised[:], in_=logs[:], func=ACT.Exp, scale=-2.0)
         nc.scalar.activation(out=warm[:, 2:3], in_=raised[:, 0:1], func=ACT.Abs_reciprocal_sqrt)
+        shrink = keep.tile([P, H], F32)
+        nc.vector.tensor_scalar_max(out=shrink[:], in0=raised[:], scalar1=1.0 / (MAX_SCALE * MAX_SCALE))
+        shrunk_eps = keep.tile([P, H], F32)
+        nc.vector.tensor_scalar(
+            out=shrunk_eps[:], in0=raised[:], scalar1=1.0 / (MAX_SCALE * MAX_SCALE), scalar2=EPS_SQUARED, op0=ALU.max, op1=ALU.mult
+        )
 
         x_words = x_sb[:].bitcast(F32)
         x_codes = keep.tile([P, TILES, PASSES, P], U32, align_bytes=64)
@@ -139,10 +150,10 @@ def tile_selfattention_pa_kernel(
                 in_=grouped,
             )
 
-        bias_sb = keep.tile([P, 2 * C], BF16)
+        bias_sb = keep.tile([P, 2 * C], F32)
 
         def spread_bias(piece):
-            spread = psum.tile([P, BANK], BF16, tag="brief", name="spread")
+            spread = psum.tile([P, BANK], F32, tag="brief", name="spread")
             nc.tensor.matmul(spread[:], lhsT=ones[:], rhs=rows[:, BANK * piece : BANK * (piece + 1)], start=True, stop=True)
             return spread
 
@@ -159,7 +170,7 @@ def tile_selfattention_pa_kernel(
                 bank = psum_k.tile([P, TOKENS, PAIR], F32, tag="held", name="bank")
             else:
                 bank = psum.tile([P, TOKENS, PAIR], F32, tag="brief", name="bank")
-            col = C * tensor + PAIR * pair
+            planes, col = (v_planes, PAIR * pair) if tensor == V else (qk_planes, C * tensor + PAIR * pair)
             piece = w_words[(tensor, pair // (PAIRS // 2))]
             inside = 2 * PAIR * (pair % (PAIRS // 2))
             for j in range(TOKENS):
@@ -170,7 +181,7 @@ def tile_selfattention_pa_kernel(
                         lhsT=x_codes[:, t, g, :].bitcast(FP8X4),
                         lhsT_scale=x_planes[:, t, g, :],
                         rhs=piece[:, g, inside : inside + 2 * PAIR].bitcast(FP4X4),
-                        rhs_scale=w_planes[:, g, col : col + PAIR],
+                        rhs_scale=planes[:, g, col : col + PAIR],
                         start=(g == 0),
                         stop=(g == PASSES - 1),
                     )
@@ -193,7 +204,7 @@ def tile_selfattention_pa_kernel(
         def squares_narrow(vector_of, sums, first, tokens):
             for j in tokens:
                 for h in range(2):
-                    unused = junk.tile([P, D], BF16, tag="unused", name="unused")
+                    unused = small.tile([P, D], BF16, tag="unused", name="unused")
                     nc.scalar.activation(out=unused[:], in_=vector_of(j, h), func=ACT.Square, accum_out=sums[:, first + 2 * j + h : first + 2 * j + h + 1])
 
         def squares_wide(bank):
@@ -212,16 +223,16 @@ def tile_selfattention_pa_kernel(
         def excess_over_eps(sums, excess, lo, hi):
             nc.scalar.activation(out=excess[:, lo:hi], in_=sums[:, lo:hi], func=ACT.Relu, bias=-EPS_SQUARED)
 
-        def inverse_norms(excess, factor):
-            nc.scalar.activation(out=factor[:], in_=excess[:], func=ACT.Abs_reciprocal_sqrt, bias=EPS_SQUARED)
+        def k_factors(excess, factor):
+            nc.scalar.activation(out=factor[:, 0:SUMS], in_=excess[:, 0:SUMS], func=ACT.Abs_reciprocal_sqrt, bias=EPS_SQUARED)
 
-        def q_multipliers(factor, pair):
-            nc.gpsimd.tensor_tensor(
-                out=factor[:, SUMS : 2 * SUMS].rearrange("p (j h) -> p j h", h=2),
-                in0=factor[:, SUMS : 2 * SUMS].rearrange("p (j h) -> p j h", h=2),
-                in1=multiplier[:, 2 * pair : 2 * pair + 2].unsqueeze(1).to_broadcast([P, TOKENS, 2]),
-                op=ALU.mult,
-            )
+        def q_factors(excess, factor, pair):
+            for h in range(2):
+                head = 2 * pair + h
+                nc.scalar.activation(
+                    out=factor[:, SUMS + h : 2 * SUMS : 2], in_=excess[:, SUMS + h : 2 * SUMS : 2], func=ACT.Abs_reciprocal_sqrt,
+                    scale=shrink[:, head : head + 1], bias=shrunk_eps[:, head : head + 1],
+                )
 
         def scale_k(bank, factor, result, half):
             nc.vector.tensor_tensor(
@@ -267,7 +278,11 @@ def tile_selfattention_pa_kernel(
         def fills(s):
             fill(K, s)
             fill(Q, s)
-            fill(V, s + LEAD_V)
+            for v in v_units(s):
+                fill(V, v)
+
+        def v_units(s):
+            return [v for v in (() if s == 0 else (0, 1) if s == 1 else (s,)) if ok(v)]
 
         grouped = keep.tile([P, TILES, 2 * K_PASS], BF16, align_bytes=64)
         spreads = {}
@@ -293,19 +308,12 @@ def tile_selfattention_pa_kernel(
                 keep_piece(BIAS_AFTER[t])
             if t in QUANTISE_AFTER:
                 quantise_some(*QUANTISE_AFTER[t])
-        for n in range(2):
-            credit(None)
         quantise_some(7, 1)
         nc.vector.tensor_copy(out=warm[:, 3:4], in_=idle_bank[:, 0:1])
-        multiplier = keep.tile([P, H], F32)
-        nc.vector.tensor_scalar_min(out=multiplier[:], in0=raised[:], scalar1=MAX_SCALE)
-        fill(K, 0)
-        fill(Q, 0)
-        for v in range(1):
-            fill(V, v)
+        fills(0)
 
         for s in range(UNITS + 2):
-            i, iv = s, s + LEAD_V
+            i = s
             if ok(i):
                 sm[("s", i)] = new_small("sums")
             if ok(i - 1):
@@ -331,15 +339,15 @@ def tile_selfattention_pa_kernel(
                 squares_narrow(lambda j, h: res[(Q, i // HALVES)][:, h, TOKENS * half + j, :], sm[("s", i)], SUMS, range(qa))
             if ok(i) and i >= NO_FOLD_FROM and i % 4 not in NARROW_K:
                 reduce_wide(sq[i], sm[("s", i)], D)
-            if ok(iv):
-                add_bias(banks[(V, iv)], res[(V, iv // HALVES)], iv % HALVES, C + PAIR * (iv // HALVES))
-                store(V, iv)
+            for v in v_units(s):
+                add_bias(banks[(V, v)], res[(V, v // HALVES)], v % HALVES, C + PAIR * (v // HALVES))
+                store(V, v)
             fills(s + 1)
             if ok(i - 1):
-                inverse_norms(sm[("e", i - 1)], sm[("f", i - 1)])
+                k_factors(sm[("e", i - 1)], sm[("f", i - 1)])
                 scale_k(banks[(K, i - 1)], sm[("f", i - 1)], res[(K, (i - 1) // HALVES)], (i - 1) % HALVES)
                 store(K, i - 1)
-                q_multipliers(sm[("f", i - 1)], (i - 1) // HALVES)
+                q_factors(sm[("e", i - 1)], sm[("f", i - 1)], (i - 1) // HALVES)
                 scale_q(res[(Q, (i - 1) // HALVES)], sm[("f", i - 1)], (i - 1) % HALVES, i - 1 >= VECTOR_Q_FROM)
                 store(Q, i - 1)
             if ok(i):

import concourse.mybir as mybir
from concourse.masks import make_identity

F32 = mybir.dt.float32
BF16 = mybir.dt.bfloat16
I32 = mybir.dt.int32
U32 = mybir.dt.uint32
U8 = mybir.dt.uint8
FP8X4 = mybir.dt.float8_e4m3fn_x4
FP4X4 = mybir.dt.float4_e2m1fn_x4
ALU = mybir.AluOpType
ACT = mybir.ActivationFunctionType
AX = mybir.AxisListType

P = 128
B, L, C, H, D = 2, 512, 1024, 16, 64
K_PASS = 512
PASSES = C // K_PASS
TILES = B * L // P
TOKENS = 4
HALVES = TILES // TOKENS
PAIR = 2 * D
PAIRS = H // 2
UNITS = HALVES * PAIRS
BANK = TOKENS * PAIR
SUMS = 2 * TOKENS
Q, K, V = 0, 1, 2
MAX_SCALE = 100.0
EPS_SQUARED = 1.0e-24

NARROW_K = (0, 2)
FOLD = True
IDLE = 384
WARM_UPS = 5
CREDITS = {0: 2, 1: None, 2: 0, 3: None, 4: 3, 5: None, 6: 1}
BIAS_AFTER = {1: 2, 3: 0, 5: 3, 7: 1}
QUANTISE_AFTER = {2: (0, 2), 4: (2, 2), 5: (4, 1), 6: (5, 1), 7: (6, 1)}
VECTOR_Q_FROM = 15
NO_FOLD_FROM = 15
VEC_COPY = (0, 2, 4, 6)

FLOPS = 2 * B * L * C * 3 * C


def tile_selfattention_pa_kernel(
    tc, x, W_qkv_words, W_qkv_scales, q_bias, v_bias, log_scale_mul, out_0, out_1, out_2
):
    nc = tc.nc
    outs = (out_0, out_1, out_2)
    with tc.tile_pool(name="keep", bufs=1) as keep, tc.tile_pool(name="regroup", bufs=4) as regroup, tc.tile_pool(
        name="stage", bufs=12
    ) as stage, tc.tile_pool(name="scratch", bufs=3) as scratch, tc.tile_pool(name="small", bufs=4) as small, tc.psum_pool(
        name="psum", bufs=5
    ) as psum, tc.psum_pool(name="psum_k", bufs=3) as psum_k, tc.manual_schedule():
        warm = keep.tile([P, 4], F32)
        nc.vector.memset(warm[:], 1.0)
        nc.scalar.activation(out=warm[:, 1:2], in_=warm[:, 0:1], func=ACT.Exp)
        ones = keep.tile([P, P], BF16)
        nc.vector.memset(ones[:], 1.0)
        idle_rhs = keep.tile([P, BANK], BF16)
        nc.gpsimd.memset(idle_rhs[:], 1.0)
        rows = keep.tile([P, 2 * C], BF16)
        nc.vector.memset(rows[:].bitcast(I32), 0)
        qk_planes = keep.tile([P, PASSES, 2 * C], U8, align_bytes=64)
        nc.vector.memset(qk_planes[:].rearrange("p g n -> p (g n)").bitcast(I32), 0)
        v_planes = keep.tile([P, PASSES, C], U8, align_bytes=64)
        nc.vector.memset(v_planes[:].rearrange("p g n -> p (g n)").bitcast(I32), 0)
        idle_bank = psum_k.tile([P, BANK], F32, tag="held", name="idle_bank")
        for n in range(WARM_UPS):
            nc.tensor.matmul(idle_bank[:], lhsT=ones[:], rhs=idle_rhs[:], start=True, stop=True)
        ident = keep.tile([P, P], F32)
        make_identity(nc, ident[:])

        x_sb = keep.tile([P, TILES, C], BF16)
        x_view = x.rearrange("b (p j) c -> p b (j c)", j=TILES)

        def load_x(first, count):
            nc.sync.dma_start(
                out=x_sb[:, first : first + count, :].rearrange("p j c -> p (j c)"),
                in_=x_view[:, :, C * first : C * (first + count)],
            )

        w_words = {}
        w_view = W_qkv_words.rearrange("g p n -> p g n")

        def load_w(tensor, half):
            first = 2 * (C * tensor + (C // 2) * half)
            piece = keep.tile([P, PASSES, C], U8, align_bytes=64, name="w_words_%d_%d" % (tensor, half))
            nc.sync.dma_start(out=piece[:].bitcast(I32), in_=w_view[:, :, first : first + C].bitcast(I32))
            w_words[(tensor, half)] = piece

        def load_planes(planes, first, count):
            for r in range(4):
                nc.sync.dma_start(
                    out=planes[r:P:32, :, :].bitcast(I32),
                    in_=W_qkv_scales[:, r:16:4, first : first + count].rearrange("g q n -> q g n").bitcast(I32),
                )

        logs = keep.tile([P, H], BF16)
        nc.sync.dma_start(out=logs[:], in_=log_scale_mul.rearrange("a h b c -> (a h b c)").partition_broadcast(P))
        load_x(0, 1)
        load_x(1, 1)
        nc.sync.dma_start(out=rows[0:1, 0:C], in_=q_bias.rearrange("(o n) -> o n", o=1))
        nc.sync.dma_start(out=rows[0:1, C : 2 * C], in_=v_bias.rearrange("(o n) -> o n", o=1))
        load_x(2, 2)
        load_x(4, 2)
        load_x(6, 1)
        load_x(7, 1)
        load_planes(qk_planes, 0, 2 * C)
        load_w(K, 0)
        load_w(Q, 0)
        load_planes(v_planes, 2 * C, C)
        load_w(V, 0)
        load_w(K, 1)
        load_w(Q, 1)
        load_w(V, 1)
        raised = keep.tile([P, H], F32)
        nc.scalar.activation(out=raised[:], in_=logs[:], func=ACT.Exp, scale=-2.0)
        nc.scalar.activation(out=warm[:, 2:3], in_=raised[:, 0:1], func=ACT.Abs_reciprocal_sqrt)
        shrink = keep.tile([P, H], F32)
        nc.vector.tensor_scalar_max(out=shrink[:], in0=raised[:], scalar1=1.0 / (MAX_SCALE * MAX_SCALE))
        shrunk_eps = keep.tile([P, H], F32)
        nc.vector.tensor_scalar(
            out=shrunk_eps[:], in0=raised[:], scalar1=1.0 / (MAX_SCALE * MAX_SCALE), scalar2=EPS_SQUARED, op0=ALU.max, op1=ALU.mult
        )

        x_words = x_sb[:].bitcast(F32)
        x_codes = keep.tile([P, TILES, PASSES, P], U32, align_bytes=64)
        x_planes = keep.tile([P, TILES, PASSES, P], U8, align_bytes=64)

        def flip(t):
            flipped = psum.tile([P, PASSES, 2, P], F32, tag="brief", name="flipped")
            for g in range(PASSES):
                for u in range(2):
                    nc.tensor.transpose(flipped[:, g, u, :], x_words[:, t, 256 * g + u : 256 * (g + 1) : 2], ident[:])
            return flipped

        def regroup_x(flipped, grouped, on_vector):
            target = grouped.bitcast(F32).rearrange("p (g m u) -> p g m u", g=PASSES, u=2)
            source = flipped[:].rearrange("p g u m -> p g m u")
            if on_vector:
                nc.vector.tensor_copy(out=target, in_=source)
            else:
                nc.scalar.copy(out=target, in_=source)

        def quantise(t, count, grouped):
            nc.vector.quantize_mx(
                out=x_codes[:, t : t + count, :, :].rearrange("p t g m -> p (t g m)").bitcast(FP8X4),
                scales=x_planes[:, t : t + count, :, :].rearrange("p t g m -> p (t g m)"),
                in_=grouped,
            )

        bias_sb = keep.tile([P, 2 * C], F32)

        def spread_bias(piece):
            spread = psum.tile([P, BANK], F32, tag="brief", name="spread")
            nc.tensor.matmul(spread[:], lhsT=ones[:], rhs=rows[:, BANK * piece : BANK * (piece + 1)], start=True, stop=True)
            return spread

        def keep_bias(piece, spread, on_vector):
            if on_vector:
                nc.vector.tensor_copy(out=bias_sb[:, BANK * piece : BANK * (piece + 1)], in_=spread[:])
            else:
                nc.scalar.copy(out=bias_sb[:, BANK * piece : BANK * (piece + 1)], in_=spread[:])


        def project(tensor, i):
            pair, half = i // HALVES, i % HALVES
            if tensor == K:
                bank = psum_k.tile([P, TOKENS, PAIR], F32, tag="held", name="bank")
            else:
                bank = psum.tile([P, TOKENS, PAIR], F32, tag="brief", name="bank")
            planes, col = (v_planes, PAIR * pair) if tensor == V else (qk_planes, C * tensor + PAIR * pair)
            piece = w_words[(tensor, pair // (PAIRS // 2))]
            inside = 2 * PAIR * (pair % (PAIRS // 2))
            for j in range(TOKENS):
                t = TOKENS * half + j
                for g in range(PASSES):
                    nc.tensor.matmul_mx(
                        out=bank[:, j, :],
                        lhsT=x_codes[:, t, g, :].bitcast(FP8X4),
                        lhsT_scale=x_planes[:, t, g, :],
                        rhs=piece[:, g, inside : inside + 2 * PAIR].bitcast(FP4X4),
                        rhs_scale=planes[:, g, col : col + PAIR],
                        start=(g == 0),
                        stop=(g == PASSES - 1),
                    )
            return bank

        def in_bank_order(result, half):
            return result[:, :, TOKENS * half : TOKENS * (half + 1), :].rearrange("p h j d -> p j h d")

        def by_head(bank):
            return bank[:].rearrange("p j (h d) -> p j h d", h=2)

        def add_bias(bank, result, half, first):
            nc.vector.tensor_tensor(
                out=in_bank_order(result, half),
                in0=by_head(bank),
                in1=bias_sb[:, first : first + PAIR].rearrange("p (h d) -> p h d", h=2).unsqueeze(1).to_broadcast([P, TOKENS, 2, D]),
                op=ALU.add,
            )

        def squares_narrow(vector_of, sums, first, tokens):
            for j in tokens:
                for h in range(2):
                    unused = small.tile([P, D], BF16, tag="unused", name="unused")
                    nc.scalar.activation(out=unused[:], in_=vector_of(j, h), func=ACT.Square, accum_out=sums[:, first + 2 * j + h : first + 2 * j + h + 1])

        def squares_wide(bank):
            squared = scratch.tile([P, SUMS, D], F32, tag="squared", name="squared")
            nc.scalar.activation(out=squared[:].rearrange("p s d -> p (s d)"), in_=bank[:].rearrange("p j n -> p (j n)"), func=ACT.Square)
            return squared

        def fold_wide(squared):
            nc.gpsimd.tensor_tensor(
                out=squared[:, :, 0 : D // 2], in0=squared[:, :, 0 : D // 2], in1=squared[:, :, D // 2 : D], op=ALU.add
            )

        def reduce_wide(squared, sums, width):
            nc.vector.tensor_reduce(out=sums[:, 0:SUMS], in_=squared[:, :, 0:width], axis=AX.X, op=ALU.add)

        def excess_over_eps(sums, excess, lo, hi):
            nc.scalar.activation(out=excess[:, lo:hi], in_=sums[:, lo:hi], func=ACT.Relu, bias=-EPS_SQUARED)

        def k_factors(excess, factor):
            nc.scalar.activation(out=factor[:, 0:SUMS], in_=excess[:, 0:SUMS], func=ACT.Abs_reciprocal_sqrt, bias=EPS_SQUARED)

        def q_factors(excess, factor, pair):
            for h in range(2):
                head = 2 * pair + h
                nc.scalar.activation(
                    out=factor[:, SUMS + h : 2 * SUMS : 2], in_=excess[:, SUMS + h : 2 * SUMS : 2], func=ACT.Abs_reciprocal_sqrt,
                    scale=shrink[:, head : head + 1], bias=shrunk_eps[:, head : head + 1],
                )

        def scale_k(bank, factor, result, half):
            nc.vector.tensor_tensor(
                out=in_bank_order(result, half),
                in0=by_head(bank),
                in1=factor[:, 0:SUMS].rearrange("p (j h) -> p j h", h=2).unsqueeze(3).to_broadcast([P, TOKENS, 2, D]),
                op=ALU.mult,
            )

        def scale_q(result, factor, half, on_vector):
            engine = nc.vector if on_vector else nc.gpsimd
            engine.tensor_tensor(
                out=result[:, :, TOKENS * half : TOKENS * (half + 1), :],
                in0=result[:, :, TOKENS * half : TOKENS * (half + 1), :],
                in1=factor[:, SUMS : 2 * SUMS].rearrange("p (j h) -> p h j", h=2).unsqueeze(3).to_broadcast([P, 2, TOKENS, D]),
                op=ALU.mult,
            )

        def store(tensor, i):
            pair, half = i // HALVES, i % HALVES
            if half == HALVES - 1:
                view = outs[tensor].rearrange("b h (p j) d -> h p b (j d)", j=TILES)
                for h in range(2):
                    nc.sync.dma_start(out=view[2 * pair + h], in_=res[(tensor, pair)][:, h, :, :].rearrange("p j d -> p (j d)"))

        def new_small(tag):
            t = small.tile([P, 2 * SUMS], F32, tag=tag, name=tag)
            return t

        flipped = [None] * TILES
        banks, res, sm, sq = {}, {}, {}, {}

        def ok(i):
            return 0 <= i < UNITS

        def fill(tensor, i):
            if ok(i):
                banks[(tensor, i)] = project(tensor, i)
                if i % HALVES == 0:
                    result = stage.tile([P, 2, TILES, D], F32, tag="result", name="result")
                    res[(tensor, i // HALVES)] = result

        def fills(s):
            fill(K, s)
            fill(Q, s)
            for v in v_units(s):
                fill(V, v)

        def v_units(s):
            return [v for v in (() if s == 0 else (0, 1) if s == 1 else (s,)) if ok(v)]

        grouped = keep.tile([P, TILES, 2 * K_PASS], BF16, align_bytes=64)
        spreads = {}

        def credit(piece):
            if piece is None:
                nc.tensor.matmul(idle_bank[:, 0:IDLE], lhsT=ones[:], rhs=idle_rhs[:, 0:IDLE], start=True, stop=True)
            else:
                spreads[piece] = spread_bias(piece)

        def keep_piece(piece):
            keep_bias(piece, spreads[piece], False)

        def quantise_some(t, count):
            quantise(t, count, grouped[:, t : t + count, :].rearrange("p t c -> p (t c)"))

        for t in range(TILES):
            flipped[t] = flip(t)
            if t in CREDITS:
                credit(CREDITS[t])
            regroup_x(flipped[t], grouped[:, t, :], t in VEC_COPY)
            if t in BIAS_AFTER:
                keep_piece(BIAS_AFTER[t])
            if t in QUANTISE_AFTER:
                quantise_some(*QUANTISE_AFTER[t])
        quantise_some(7, 1)
        nc.vector.tensor_copy(out=warm[:, 3:4], in_=idle_bank[:, 0:1])
        fills(0)

        for s in range(UNITS + 2):
            i = s
            if ok(i):
                sm[("s", i)] = new_small("sums")
            if ok(i - 1):
                sm[("e", i - 1)] = new_small("excess")
                sm[("f", i - 1)] = new_small("factor")
            if ok(i):
                add_bias(banks[(Q, i)], res[(Q, i // HALVES)], i % HALVES, PAIR * (i // HALVES))
                if i % 4 in NARROW_K:
                    squares_narrow(lambda j, h: banks[(K, i)][:, j, D * h : D * (h + 1)], sm[("s", i)], 0, range(2))
                else:
                    sq[i] = squares_wide(banks[(K, i)])
                    if FOLD and i < NO_FOLD_FROM:
                        fold_wide(sq[i])
            if ok(i - 1):
                excess_over_eps(sm[("s", i - 1)], sm[("e", i - 1)], 0, 2 * SUMS)
            if ok(i):
                half = i % HALVES
                if i % 4 in NARROW_K:
                    squares_narrow(lambda j, h: banks[(K, i)][:, j, D * h : D * (h + 1)], sm[("s", i)], 0, range(2, TOKENS))
                    qa = 0
                else:
                    qa = 1
                squares_narrow(lambda j, h: res[(Q, i // HALVES)][:, h, TOKENS * half + j, :], sm[("s", i)], SUMS, range(qa))
            if ok(i) and i >= NO_FOLD_FROM and i % 4 not in NARROW_K:
                reduce_wide(sq[i], sm[("s", i)], D)
            for v in v_units(s):
                add_bias(banks[(V, v)], res[(V, v // HALVES)], v % HALVES, C + PAIR * (v // HALVES))
                store(V, v)
            fills(s + 1)
            if ok(i - 1):
                k_factors(sm[("e", i - 1)], sm[("f", i - 1)])
                scale_k(banks[(K, i - 1)], sm[("f", i - 1)], res[(K, (i - 1) // HALVES)], (i - 1) % HALVES)
                store(K, i - 1)
                q_factors(sm[("e", i - 1)], sm[("f", i - 1)], (i - 1) // HALVES)
                scale_q(res[(Q, (i - 1) // HALVES)], sm[("f", i - 1)], (i - 1) % HALVES, i - 1 >= VECTOR_Q_FROM)
                store(Q, i - 1)
            if ok(i):
                squares_narrow(lambda j, h: res[(Q, i // HALVES)][:, h, TOKENS * half + j, :], sm[("s", i)], SUMS, range(qa, TOKENS))
            if ok(i) and i < NO_FOLD_FROM and i % 4 not in NARROW_K:
                reduce_wide(sq[i], sm[("s", i)], D // 2 if FOLD else D)
